import numpy as np
import ml_dtypes


def mxq(x, axis, fmt="e4m3"):
    dtype, down = {"e4m3": (ml_dtypes.float8_e4m3fn, 7), "e5m2": (ml_dtypes.float8_e5m2, 14)}[fmt]
    v = np.moveaxis(np.asarray(x, np.float32).astype(ml_dtypes.bfloat16).astype(np.float64), axis, -1)
    blocks = v.reshape(v.shape[:-1] + (-1, 32))
    amax = np.abs(blocks).max(-1, keepdims=True)
    byte = np.maximum(np.where(amax > 0, np.frexp(amax)[1] - 1 + 127, 0) - down, 1)
    scale = np.exp2(byte - 127.0)
    codes = (blocks / scale).astype(np.float32).astype(dtype).astype(np.float64)
    return np.moveaxis((codes * scale).reshape(v.shape), -1, axis)


WIDE = False


def mx_kscale(k):
    if not WIDE:
        return np.ones(k)
    levels = np.array([10, -10, 5, -5, 0])
    if k % 512:
        return np.exp2(np.random.permutation(np.resize(levels, k // 32))).repeat(32)
    a = np.empty((k // 512, 16))
    for p in range(k // 512):
        a[p, :8] = np.random.permutation(np.resize(levels, 8))
        for g in range(8):
            far = levels[np.abs(levels - a[p, g]) >= 10]
            a[p, g + 8] = far[np.random.randint(len(far))]
    return np.exp2(a.ravel()).repeat(32)


BF16 = ml_dtypes.bfloat16


def bf(x):
    return np.asarray(x, np.float32).astype(BF16)


def f64(x):
    return np.asarray(x).astype(np.float64)


B, S, H, D = 2, 512, 16, 64
E = H * D
HALF = D // 2


def rotate_half(u):
    u1, u2 = np.split(u, 2, axis=-1)
    return np.concatenate([-u2, u1], axis=-1)


def apply_rope(t, sin, cos):
    x1, x2 = np.split(t, 2, axis=-1)
    x_rot = x1 * cos + rotate_half(x1) * sin
    return np.concatenate([x_rot, x2], axis=-1)


def setup_inputs():
    s = mx_kscale(E)
    th = np.random.uniform(0.0, 2.0 * np.pi, (S, HALF))
    return {"x": bf(np.random.standard_normal((B, S, E)) * s),
            "W_qkv": bf(np.random.standard_normal((E, 3 * E)) / np.sqrt(E) / s[:, None]),
            "b_qkv": bf(np.random.standard_normal(3 * E) * 0.2),
            "sin_tab": bf(np.sin(th)),
            "cos_tab": bf(np.cos(th))}


def reference(x, W_qkv, b_qkv, sin_tab, cos_tab):
    qkv = (mxq(f64(x), 2, "e4m3") @ mxq(f64(W_qkv), 0, "e4m3")) + f64(b_qkv)
    q, k, v = np.split(qkv, 3, axis=-1)
    q = q.reshape(B, S, H, D)
    k = k.reshape(B, S, H, D)
    v = v.reshape(B, S, H, D)
    sin = f64(sin_tab)[None, :, None, :]
    cos = f64(cos_tab)[None, :, None, :]
    q_rot = apply_rope(q, sin, cos)
    k_rot = apply_rope(k, sin, cos)
    return q_rot, k_rot, v

@@ -1,0 +1,352 @@
+from contextlib import ExitStack
+
+import concourse.mybir as mybir
+from concourse.masks import make_identity
+
+F32 = mybir.dt.float32
+BF16 = mybir.dt.bfloat16
+U32 = mybir.dt.uint32
+U8 = mybir.dt.uint8
+FP8X4 = mybir.dt.float8_e4m3fn_x4
+ALU = mybir.AluOpType
+ACT = mybir.ActivationFunctionType
+
+P = 128
+B, S, H, D = 2, 512, 16, 64
+E = H * D
+R = D // 2
+HALF = R // 2
+TILES = S // P
+PASSES = E // (4 * P)
+BANK = 512
+HEADS = BANK // D
+FLOPS = 2 * B * S * E * 3 * E
+
+CHUNKS = ((0, 0), (0, 1), (1, 0), (1, 1), (2, 0), (2, 1))
+V_CHUNKS = (4, 5)
+UNITS = 4 * TILES
+V_STEPS = 16
+V_PAIRS = V_STEPS // 2
+FEATURE_TILES = BANK // P
+STEPS_PER_CHUNK = B * FEATURE_TILES
+
+
+def vector_adds_turned_bias(unit):
+    return unit % 2 == 0 or unit == UNITS - 1
+
+
+def tile_improvedattention_pa_kernel(tc, x, W_qkv, b_qkv, sin_tab, cos_tab, out_0, out_1, out_2):
+    nc = tc.nc
+    outs = (out_0, out_1, out_2)
+    with ExitStack() as ctx:
+        ctx.enter_context(tc.manual_schedule())
+        keep = ctx.enter_context(tc.tile_pool(name="keep", bufs=1))
+        x_grouped_pool = ctx.enter_context(tc.tile_pool(name="x_grouped", bufs=2))
+        w_grouped_pool = ctx.enter_context(tc.tile_pool(name="w_grouped", bufs=3))
+        products_pool = ctx.enter_context(tc.tile_pool(name="products", bufs=4))
+        unit_out_pool = ctx.enter_context(tc.tile_pool(name="unit_out", bufs=5))
+        turned_bias_pool = ctx.enter_context(tc.tile_pool(name="turned_bias", bufs=3))
+        v_T_pool = ctx.enter_context(tc.tile_pool(name="v_T", bufs=4))
+        v_out_pool = ctx.enter_context(tc.tile_pool(name="v_out", bufs=2))
+        psum = ctx.enter_context(tc.psum_pool(name="psum", bufs=8))
+
+        x_raw = [keep.tile([P, B, E], BF16, name="x_raw%d" % j) for j in range(TILES)]
+        w_raw = [keep.tile([P, 4 * PASSES, BANK], BF16, name="w_raw%d" % c) for c in range(len(CHUNKS))]
+        w_codes = [keep.tile([P, PASSES, BANK], U32, name="w_codes%d" % c, align_bytes=64) for c in range(len(CHUNKS))]
+        w_scales = [keep.tile([P, PASSES, BANK], U8, name="w_scales%d" % c, align_bytes=64) for c in range(len(CHUNKS))]
+        x_codes = keep.tile([P, B, PASSES, TILES, P], U32, align_bytes=64)
+        x_scales = keep.tile([P, B, PASSES, TILES, P], U8, align_bytes=64)
+        cos16 = keep.tile([P, TILES, R], BF16)
+        sin16 = keep.tile([P, TILES, R], BF16)
+        factors = keep.tile([P, TILES, 2, R], F32)
+        table = keep.tile([P, TILES, P], BF16)
+        table_T = keep.tile([P, TILES, P], BF16)
+        bias_rows = keep.tile([P, P], BF16)
+        bias_masked = keep.tile([P, 2 * H, R], BF16)
+        mask = keep.tile([P, R], F32)
+        selector = keep.tile([P, P], BF16)
+        pass_bias = keep.tile([P, 2 * H, R], F32)
+        v_bias = keep.tile([P, 2 * FEATURE_TILES], F32)
+        ident = keep.tile([P, P], F32)
+        ident16 = keep.tile([P, P], BF16)
+
+        nc.vector.memset(bias_rows[:], 0.0)
+        nc.vector.memset(table[:], 0.0)
+        nc.vector.memset(selector[:], 0.0)
+        nc.vector.memset(selector[2 * R:3 * R, :], 1.0)
+        make_identity(nc, ident[:])
+
+        def load_x(j):
+            nc.sync.dma_start(out=x_raw[j][:], in_=x[:, j * P:(j + 1) * P, :].rearrange("b p k -> p b k"))
+
+        def load_w(c, passes):
+            c0 = CHUNKS[c][0] * E + CHUNKS[c][1] * BANK
+            for g in passes:
+                nc.sync.dma_start(
+                    out=w_raw[c][:, 4 * g:4 * g + 4, :],
+                    in_=W_qkv[4 * P * g:4 * P * (g + 1), c0:c0 + BANK].rearrange("(p t) c -> p t c", t=4),
+                )
+
+        nc.sync.dma_start(out=cos16[:], in_=cos_tab.rearrange("(t p) j -> p t j", p=P))
+        nc.sync.dma_start(out=sin16[:], in_=sin_tab.rearrange("(t p) j -> p t j", p=P))
+        qk_bias = b_qkv[0:2 * E].rearrange("(r d) -> r d", d=D)
+        nc.sync.dma_start(out=bias_rows[0:2 * H, 0:R], in_=qk_bias[:, 0:R])
+        nc.sync.dma_start(out=bias_rows[0:2 * H, R:2 * R], in_=qk_bias[:, 0:R])
+        nc.sync.dma_start(out=bias_rows[0:2 * H, 2 * R:3 * R], in_=qk_bias[:, R:D])
+        nc.sync.dma_start(
+            out=bias_rows[2 * H:2 * H + 2 * FEATURE_TILES, :], in_=b_qkv[2 * E:3 * E].rearrange("(r c) -> r c", c=P)
+        )
+        load_w(0, (0,))
+        load_x(0)
+        load_w(0, (1,))
+        load_x(1)
+        load_w(4, range(PASSES))
+        load_x(2)
+        load_x(3)
+        for c in (1, 2, 5, 3):
+            load_w(c, range(PASSES))
+
+        nc.vector.tensor_copy(out=ident16[:], in_=ident[:])
+        nc.vector.tensor_tensor(out=mask[:], in0=ident[:, 0:R], in1=ident[:, 2 * R:3 * R], op=ALU.add)
+        nc.vector.tensor_tensor(
+            out=mask[:, 0:HALF], in0=mask[:, 0:HALF], in1=ident[:, R + HALF:2 * R], op=ALU.add
+        )
+        nc.vector.tensor_tensor(out=mask[:, HALF:R], in0=mask[:, HALF:R], in1=ident[:, R:R + HALF], op=ALU.add)
+        nc.vector.tensor_copy(out=factors[:, :, 0, :], in_=cos16[:])
+        nc.vector.tensor_copy(out=factors[:, :, 1, 0:HALF], in_=sin16[:, :, HALF:R])
+        nc.vector.tensor_scalar_mul(out=factors[:, :, 1, HALF:R], in0=sin16[:, :, 0:HALF], scalar1=-1.0)
+        nc.vector.tensor_copy(out=table[:, :, 0:2 * R], in_=factors[:].rearrange("p t c j -> p t (c j)"))
+
+        def mx_product(out, lhsT, lhsT_scale, rhs, rhs_scale):
+            for g in range(PASSES):
+                nc.tensor.matmul_mx(
+                    out=out,
+                    lhsT=lhsT(g).bitcast(FP8X4),
+                    lhsT_scale=lhsT_scale(g),
+                    rhs=rhs(g).bitcast(FP8X4),
+                    rhs_scale=rhs_scale(g),
+                    start=(g == 0),
+                    stop=(g == PASSES - 1),
+                )
+
+        def transpose_x(j):
+            grouped = x_grouped_pool.tile([P, B, PASSES, P, 4], BF16, name="x_grouped", tag="x_grouped", align_bytes=64)
+            banks = []
+            for b in range(B):
+                words = x_raw[j][:, b, :].bitcast(F32)
+                bank = psum.tile([P, 2 * PASSES, P], F32, name="x_bank", tag="bank")
+                for g in range(PASSES):
+                    for u in range(2):
+                        nc.tensor.transpose(
+                            bank[:, 2 * g + u, :], words[:, 2 * P * g + u:2 * P * (g + 1):2], ident[:]
+                        )
+                banks.append(bank)
+            for b in range(B):
+                nc.scalar.copy(
+                    out=grouped[:].bitcast(F32)[:, b], in_=banks[b][:].rearrange("p (g u) r -> p g r u", u=2)
+                )
+            return grouped
+
+        def quantise_x(j, grouped):
+            for b in range(B):
+                for g in range(PASSES):
+                    nc.vector.quantize_mx(
+                        out=x_codes[:, b, g, j, :].bitcast(FP8X4),
+                        scales=x_scales[:, b, g, j, :],
+                        in_=grouped[:, b, g].rearrange("p r t -> p (r t)"),
+                    )
+
+        w_grouped = {}
+
+        def regroup_w(copy, pieces, c, g):
+            if g == 0:
+                w_grouped[c] = w_grouped_pool.tile(
+                    [P, PASSES, BANK, 4], BF16, name="w_grouped", tag="w_grouped", align_bytes=64
+                )
+            width = BANK // pieces
+            for i in range(pieces):
+                copy(
+                    out=w_grouped[c][:, g, i * width:(i + 1) * width, :].rearrange("p (c i) t -> p c t i", i=4),
+                    in_=w_raw[c][:, 4 * g:4 * g + 4, i * width:(i + 1) * width].rearrange("p t (c i) -> p c t i", i=4),
+                )
+
+        def quantise_w(c):
+            nc.vector.quantize_mx(
+                out=w_codes[c][:].rearrange("p g c -> p (g c)").bitcast(FP8X4),
+                scales=w_scales[c][:].rearrange("p g c -> p (g c)"),
+                in_=w_grouped[c][:].rearrange("p g c t -> p (g c t)"),
+            )
+
+        def unit_products(unit):
+            c, j = unit // TILES, unit % TILES
+            head0 = CHUNKS[c][0] * H + CHUNKS[c][1] * HEADS
+            turned_bank = psum.tile([P, HEADS, R], F32, name="turned_bank", tag="bank")
+            nc.tensor.matmul(
+                out=turned_bank[:].rearrange("p h j -> p (h j)"),
+                lhsT=table_T[:, j, :],
+                rhs=bias_masked[:, head0:head0 + HEADS, :].rearrange("p r j -> p (r j)"),
+                start=True,
+                stop=True,
+            )
+            banks = []
+            for b in range(B):
+                bank = psum.tile([P, BANK], F32, name="unit_bank", tag="bank")
+                mx_product(
+                    bank[:],
+                    lambda g: x_codes[:, b, g, j, :],
+                    lambda g: x_scales[:, b, g, j, :],
+                    lambda g: w_codes[c][:, g, :],
+                    lambda g: w_scales[c][:, g, :],
+                )
+                banks.append(bank)
+            turned_bias = turned_bank
+            if not vector_adds_turned_bias(unit):
+                turned_bias = turned_bias_pool.tile([P, HEADS, R], F32, name="turned_bias", tag="turned_bias")
+                nc.scalar.copy(out=turned_bias[:], in_=turned_bank[:])
+            return banks, turned_bias
+
+        def unit_finish(unit, banks, turned_bias):
+            c, j = unit // TILES, unit % TILES
+            which, half = CHUNKS[c]
+            head0 = which * H + half * HEADS
+            products = products_pool.tile([P, B, HEADS, 2, R], F32, name="products", tag="products")
+            result = unit_out_pool.tile([P, B, BANK], F32, name="unit_out", tag="unit_out")
+            for b in range(B):
+                heads = banks[b][:].rearrange("p (h d) -> p h d", d=D)
+                nc.vector.tensor_tensor(
+                    out=products[:, b],
+                    in0=heads[:, :, 0:R].unsqueeze(2).to_broadcast([P, HEADS, 2, R]),
+                    in1=factors[:, j].unsqueeze(1).to_broadcast([P, HEADS, 2, R]),
+                    op=ALU.mult,
+                )
+                nc.vector.tensor_tensor(
+                    out=result[:, b, :].rearrange("p (h d) -> p h d", d=D)[:, :, R:D],
+                    in0=heads[:, :, R:D],
+                    in1=pass_bias[:, head0:head0 + HEADS, :],
+                    op=ALU.add,
+                )
+            for_both = turned_bias[:].unsqueeze(1).to_broadcast([P, B, HEADS, R])
+            if vector_adds_turned_bias(unit):
+                with_cos = products[:, :, :, 0, :]
+                nc.vector.tensor_tensor(out=with_cos, in0=with_cos, in1=for_both, op=ALU.add)
+            heads = result[:].rearrange("p b (h d) -> p (b h) d", d=D)
+            pairs = products[:].rearrange("p b h c j -> p (b h) c j")
+            nc.gpsimd.tensor_tensor(
+                out=heads[:, :, 0:HALF], in0=pairs[:, :, 0, 0:HALF], in1=pairs[:, :, 1, HALF:R], op=ALU.add
+            )
+            nc.gpsimd.tensor_tensor(
+                out=heads[:, :, HALF:R], in0=pairs[:, :, 0, HALF:R], in1=pairs[:, :, 1, 0:HALF], op=ALU.add
+            )
+            if not vector_adds_turned_bias(unit):
+                turned = result[:].rearrange("p b (h d) -> p b h d", d=D)[:, :, :, 0:R]
+                nc.gpsimd.tensor_tensor(out=turned, in0=turned, in1=for_both, op=ALU.add)
+            dst = outs[which].rearrange("b s h d -> s b (h d)")
+            nc.sync.dma_start(out=dst[j * P:(j + 1) * P, :, half * BANK:(half + 1) * BANK], in_=result[:])
+
+        v_T = {}
+        v_out = {}
+
+        def v_front(pair):
+            banks = []
+            for n in (2 * pair, 2 * pair + 1):
+                c, b, f = V_CHUNKS[n // STEPS_PER_CHUNK], (n // FEATURE_TILES) % B, n % FEATURE_TILES
+                bank = psum.tile([P, BANK], F32, name="v_bank", tag="bank")
+                mx_product(
+                    bank[:],
+                    lambda g: w_codes[c][:, g, f * P:(f + 1) * P],
+                    lambda g: w_scales[c][:, g, f * P:(f + 1) * P],
+                    lambda g: x_codes[:, b, g].rearrange("p j r -> p (j r)"),
+                    lambda g: x_scales[:, b, g].rearrange("p j r -> p (j r)"),
+                )
+                banks.append(bank)
+            for n in (2 * pair, 2 * pair + 1):
+                column = CHUNKS[V_CHUNKS[n // STEPS_PER_CHUNK]][1] * FEATURE_TILES + n % FEATURE_TILES
+                v_T[n] = v_T_pool.tile([P, BANK], F32, name="v_T", tag="v_T")
+                nc.scalar.activation(
+                    out=v_T[n][:], in_=banks[n % 2][:], func=ACT.Identity, bias=v_bias[:, column:column + 1], scale=1.0
+                )
+
+        def v_back(pair):
+            banks = []
+            for n in (2 * pair, 2 * pair + 1):
+                bank = psum.tile([P, TILES, P], F32, name="v_back", tag="bank")
+                for j in range(TILES):
+                    nc.tensor.transpose(bank[:, j, :], v_T[n][:, j * P:(j + 1) * P], ident[:])
+                banks.append(bank)
+            for n in (2 * pair, 2 * pair + 1):
+                quarter, f = n // FEATURE_TILES, n % FEATURE_TILES
+                if f == 0:
+                    v_out[quarter] = v_out_pool.tile([P, TILES, BANK], F32, name="v_out", tag="v_out")
+                nc.scalar.copy(out=v_out[quarter][:, :, f * P:(f + 1) * P], in_=banks[n % 2][:])
+                if f == FEATURE_TILES - 1:
+                    half, b = CHUNKS[V_CHUNKS[quarter // B]][1], quarter % B
+                    dst = out_2.rearrange("b (j p) h d -> p b j (h d)", p=P)
+                    nc.sync.dma_start(out=dst[:, b, :, half * BANK:(half + 1) * BANK], in_=v_out[quarter][:])
+
+        table_bank = psum.tile([P, TILES, P], BF16, name="table_bank", tag="bank")
+        for t in range(TILES):
+            nc.tensor.transpose(table_bank[:, t, :], table[:, t, :], ident16[:])
+        bias_bank = psum.tile([P, P], BF16, name="bias_bank", tag="bank")
+        nc.tensor.transpose(bias_bank[:], bias_rows[:], ident16[:])
+        nc.scalar.copy(out=table_T[:], in_=table_bank[:])
+        nc.vector.tensor_tensor(
+            out=bias_masked[:],
+            in0=bias_bank[:, 0:2 * H].unsqueeze(2).to_broadcast([P, 2 * H, R]),
+            in1=mask[:].unsqueeze(1).to_broadcast([P, 2 * H, R]),
+            op=ALU.mult,
+        )
+        nc.vector.tensor_copy(out=v_bias[:], in_=bias_bank[:, 2 * H:2 * H + 2 * FEATURE_TILES])
+        x_grouped = {0: transpose_x(0)}
+        pass_banks = []
+        for w in range(2):
+            pass_bank = psum.tile([P, H, R], F32, name="pass_bank", tag="bank")
+            nc.tensor.matmul(
+                out=pass_bank[:].rearrange("p h j -> p (h j)"),
+                lhsT=selector[:],
+                rhs=bias_masked[:, w * H:(w + 1) * H, :].rearrange("p r j -> p (r j)"),
+                start=True,
+                stop=True,
+            )
+            pass_banks.append(pass_bank)
+        for w in range(2):
+            nc.scalar.copy(out=pass_bias[:, w * H:(w + 1) * H, :], in_=pass_banks[w][:])
+        for g in range(PASSES):
+            regroup_w(nc.vector.tensor_copy, 1, 0, g)
+        quantise_x(0, x_grouped[0])
+        quantise_w(0)
+        x_grouped[1] = transpose_x(1)
+        quantise_x(1, x_grouped[1])
+
+        scalar_passes = [(c, g) for c in (4, 1, 2, 5, 3) for g in range(PASSES)]
+        v_parts = []
+        for pair in range(V_PAIRS + 1):
+            if pair < V_PAIRS:
+                v_parts.append(("front", pair))
+            if pair >= 1:
+                v_parts.append(("back", pair - 1))
+        quantise_after = {3: (4, 1), 6: (2,), 8: (5,), 10: (3,)}
+        placed = 0
+        for unit in range(UNITS):
+            banks, turned_bias = unit_products(unit)
+            if unit == 1:
+                for j in (2, 3):
+                    x_grouped[j] = transpose_x(j)
+            for i in range((1, 1, 2, 2)[unit] if unit < 4 else 0):
+                regroup_w(nc.scalar.copy, 2, scalar_passes[0][0], scalar_passes[0][1])
+                scalar_passes = scalar_passes[1:]
+            while placed < min(len(v_parts), (3 * (unit - 4) + 1) // 2):
+                part, pair = v_parts[placed]
+                if part == "front":
+                    v_front(pair)
+                else:
+                    v_back(pair)
+                if scalar_passes and placed % 2 == 0:
+                    regroup_w(nc.scalar.copy, 2, scalar_passes[0][0], scalar_passes[0][1])
+                    scalar_passes = scalar_passes[1:]
+                placed += 1
+            unit_finish(unit, banks, turned_bias)
+            if unit == 1:
+                for j in (2, 3):
+                    quantise_x(j, x_grouped[j])
+            for c in quantise_after.get(unit, ()):
+                quantise_w(c)

@@ -19,20 +19,10 @@ HALF = R // 2
 TILES = S // P
 PASSES = E // (4 * P)
 BANK = 512
-HEADS = BANK // D
+FT = 4
+HG = H // 2
 FLOPS = 2 * B * S * E * 3 * E
-
-CHUNKS = ((0, 0), (0, 1), (1, 0), (1, 1), (2, 0), (2, 1))
-V_CHUNKS = (4, 5)
-UNITS = 4 * TILES
-V_STEPS = 16
-V_PAIRS = V_STEPS // 2
-FEATURE_TILES = BANK // P
-STEPS_PER_CHUNK = B * FEATURE_TILES
-
-
-def vector_adds_turned_bias(unit):
-    return unit % 2 == 0 or unit == UNITS - 1
+BLOCKS = ((0, 0), (0, 1), (1, 0), (1, 1))
 
 
 def tile_improvedattention_pa_kernel(tc, x, W_qkv, b_qkv, sin_tab, cos_tab, out_0, out_1, out_2):
@@ -42,80 +32,74 @@ def tile_improvedattention_pa_kernel(tc, x, W_qkv, b_qkv, sin_tab, cos_tab, out_
         ctx.enter_context(tc.manual_schedule())
         keep = ctx.enter_context(tc.tile_pool(name="keep", bufs=1))
         x_grouped_pool = ctx.enter_context(tc.tile_pool(name="x_grouped", bufs=2))
-        w_grouped_pool = ctx.enter_context(tc.tile_pool(name="w_grouped", bufs=3))
-        products_pool = ctx.enter_context(tc.tile_pool(name="products", bufs=4))
-        unit_out_pool = ctx.enter_context(tc.tile_pool(name="unit_out", bufs=5))
-        turned_bias_pool = ctx.enter_context(tc.tile_pool(name="turned_bias", bufs=3))
-        v_T_pool = ctx.enter_context(tc.tile_pool(name="v_T", bufs=4))
-        v_out_pool = ctx.enter_context(tc.tile_pool(name="v_out", bufs=2))
-        psum = ctx.enter_context(tc.psum_pool(name="psum", bufs=8))
+        w_grouped_pool = ctx.enter_context(tc.tile_pool(name="w_grouped", bufs=2))
+        v_grouped_pool = ctx.enter_context(tc.tile_pool(name="v_grouped", bufs=2))
+        y_pool = ctx.enter_context(tc.tile_pool(name="y", bufs=10))
+        biased_pool = ctx.enter_context(tc.tile_pool(name="biased", bufs=2))
+        result_pool = ctx.enter_context(tc.tile_pool(name="result", bufs=7))
+        a_psum = ctx.enter_context(tc.psum_pool(name="a_psum", bufs=3))
+        t_psum = ctx.enter_context(tc.psum_pool(name="t_psum", bufs=2))
+        p_psum = ctx.enter_context(tc.psum_pool(name="p_psum", bufs=3))
 
-        x_raw = [keep.tile([P, B, E], BF16, name="x_raw%d" % j) for j in range(TILES)]
-        w_raw = [keep.tile([P, 4 * PASSES, BANK], BF16, name="w_raw%d" % c) for c in range(len(CHUNKS))]
-        w_codes = [keep.tile([P, PASSES, BANK], U32, name="w_codes%d" % c, align_bytes=64) for c in range(len(CHUNKS))]
-        w_scales = [keep.tile([P, PASSES, BANK], U8, name="w_scales%d" % c, align_bytes=64) for c in range(len(CHUNKS))]
+        x_raw = [[y_pool.tile([P, 2, E], BF16, name="x_raw", tag="y") for i in range(2)] for b in range(B)]
+        wq_raw = [[y_pool.tile([P, 4, BANK], BF16, name="wq_raw", tag="y") for g in range(PASSES)] for i in range(2)]
+        w_raw = {w: [keep.tile([P, 4, E], BF16, name="w_raw%d%d" % (w, g)) for g in range(PASSES)] for w in (1, 2)}
+        w_codes = [
+            [keep.tile([P, PASSES, BANK], U32, name="w_codes%d%d" % (w, i), align_bytes=64) for i in range(2)]
+            for w in range(3)
+        ]
+        w_scales = [
+            [keep.tile([P, PASSES, BANK], U8, name="w_scales%d%d" % (w, i), align_bytes=64) for i in range(2)]
+            for w in range(3)
+        ]
         x_codes = keep.tile([P, B, PASSES, TILES, P], U32, align_bytes=64)
         x_scales = keep.tile([P, B, PASSES, TILES, P], U8, align_bytes=64)
         cos16 = keep.tile([P, TILES, R], BF16)
         sin16 = keep.tile([P, TILES, R], BF16)
-        factors = keep.tile([P, TILES, 2, R], F32)
-        table = keep.tile([P, TILES, P], BF16)
-        table_T = keep.tile([P, TILES, P], BF16)
-        bias_rows = keep.tile([P, P], BF16)
-        bias_masked = keep.tile([P, 2 * H, R], BF16)
-        mask = keep.tile([P, R], F32)
-        selector = keep.tile([P, P], BF16)
-        pass_bias = keep.tile([P, 2 * H, R], F32)
-        v_bias = keep.tile([P, 2 * FEATURE_TILES], F32)
+        table = keep.tile([P, 2, TILES, 4, R], BF16)
+        table_T = keep.tile([P, 2, BANK], BF16)
+        bias_row = keep.tile([P, 3 * E], BF16)
+        ones = keep.tile([P, P], BF16)
+        turned_rows = keep.tile([P, P], BF16)
+        turned_bias = keep.tile([P, 2 * FT], F32)
+        pass_bias = keep.tile([P, 2, BANK], BF16)
+        v_bias = keep.tile([P, E], BF16)
         ident = keep.tile([P, P], F32)
         ident16 = keep.tile([P, P], BF16)
+        swap = keep.tile([P, P], F32)
 
-        nc.vector.memset(bias_rows[:], 0.0)
-        nc.vector.memset(table[:], 0.0)
-        nc.vector.memset(selector[:], 0.0)
-        nc.vector.memset(selector[2 * R:3 * R, :], 1.0)
         make_identity(nc, ident[:])
-
-        def load_x(j):
-            nc.sync.dma_start(out=x_raw[j][:], in_=x[:, j * P:(j + 1) * P, :].rearrange("b p k -> p b k"))
-
-        def load_w(c, passes):
-            c0 = CHUNKS[c][0] * E + CHUNKS[c][1] * BANK
-            for g in passes:
-                nc.sync.dma_start(
-                    out=w_raw[c][:, 4 * g:4 * g + 4, :],
-                    in_=W_qkv[4 * P * g:4 * P * (g + 1), c0:c0 + BANK].rearrange("(p t) c -> p t c", t=4),
-                )
-
-        nc.sync.dma_start(out=cos16[:], in_=cos_tab.rearrange("(t p) j -> p t j", p=P))
-        nc.sync.dma_start(out=sin16[:], in_=sin_tab.rearrange("(t p) j -> p t j", p=P))
-        qk_bias = b_qkv[0:2 * E].rearrange("(r d) -> r d", d=D)
-        nc.sync.dma_start(out=bias_rows[0:2 * H, 0:R], in_=qk_bias[:, 0:R])
-        nc.sync.dma_start(out=bias_rows[0:2 * H, R:2 * R], in_=qk_bias[:, 0:R])
-        nc.sync.dma_start(out=bias_rows[0:2 * H, 2 * R:3 * R], in_=qk_bias[:, R:D])
-        nc.sync.dma_start(
-            out=bias_rows[2 * H:2 * H + 2 * FEATURE_TILES, :], in_=b_qkv[2 * E:3 * E].rearrange("(r c) -> r c", c=P)
+        nc.vector.memset(turned_rows[:], 0.0)
+        nc.vector.memset(ones[:], 1.0)
+        nc.gpsimd.memset(bias_row[:].bitcast(U32), 0)
+        nc.scalar.dma_start(out=cos16[:], in_=cos_tab.rearrange("(p t) j -> p t j", t=TILES))
+        nc.scalar.dma_start(out=sin16[:], in_=sin_tab.rearrange("(p t) j -> p t j", t=TILES))
+        nc.scalar.dma_start(
+            out=turned_rows[0:2 * FT, :].rearrange("r (h j) -> r h j", j=R),
+            in_=b_qkv[0:2 * E].rearrange("(r h d) -> r h d", h=4, d=D)[:, :, 0:R],
         )
-        load_w(0, (0,))
-        load_x(0)
-        load_w(0, (1,))
-        load_x(1)
-        load_w(4, range(PASSES))
-        load_x(2)
-        load_x(3)
-        for c in (1, 2, 5, 3):
-            load_w(c, range(PASSES))
+        nc.scalar.dma_start(out=bias_row[0:1, :], in_=b_qkv.rearrange("(o c) -> o c", o=1))
 
-        nc.vector.tensor_copy(out=ident16[:], in_=ident[:])
-        nc.vector.tensor_tensor(out=mask[:], in0=ident[:, 0:R], in1=ident[:, 2 * R:3 * R], op=ALU.add)
-        nc.vector.tensor_tensor(
-            out=mask[:, 0:HALF], in0=mask[:, 0:HALF], in1=ident[:, R + HALF:2 * R], op=ALU.add
-        )
-        nc.vector.tensor_tensor(out=mask[:, HALF:R], in0=mask[:, HALF:R], in1=ident[:, R:R + HALF], op=ALU.add)
-        nc.vector.tensor_copy(out=factors[:, :, 0, :], in_=cos16[:])
-        nc.vector.tensor_copy(out=factors[:, :, 1, 0:HALF], in_=sin16[:, :, HALF:R])
-        nc.vector.tensor_scalar_mul(out=factors[:, :, 1, HALF:R], in0=sin16[:, :, 0:HALF], scalar1=-1.0)
-        nc.vector.tensor_copy(out=table[:, :, 0:2 * R], in_=factors[:].rearrange("p t c j -> p t (c j)"))
+        def load_x(b, i):
+            src = x[b].rearrange("(p t) k -> p t k", t=TILES)
+            nc.sync.dma_start(out=x_raw[b][i][:], in_=src[:, 2 * i:2 * i + 2, :])
+
+        def load_wq(i, g):
+            src = W_qkv[4 * P * g:4 * P * (g + 1), i * BANK:(i + 1) * BANK]
+            nc.sync.dma_start(out=wq_raw[i][g][:], in_=src.rearrange("(p t) c -> p t c", t=4))
+
+        load_x(0, 0)
+        load_wq(0, 0)
+        load_x(0, 1)
+        load_wq(0, 1)
+        load_wq(1, 0)
+        load_wq(1, 1)
+        load_x(1, 0)
+        load_x(1, 1)
+        for w in (1, 2):
+            for g in range(PASSES):
+                src = W_qkv[4 * P * g:4 * P * (g + 1), w * E:(w + 1) * E]
+                nc.sync.dma_start(out=w_raw[w][g][:], in_=src.rearrange("(p t) c -> p t c", t=4))
 
         def mx_product(out, lhsT, lhsT_scale, rhs, rhs_scale):
             for g in range(PASSES):
@@ -129,224 +113,298 @@ def tile_improvedattention_pa_kernel(tc, x, W_qkv, b_qkv, sin_tab, cos_tab, out_
                     stop=(g == PASSES - 1),
                 )
 
-        def transpose_x(j):
-            grouped = x_grouped_pool.tile([P, B, PASSES, P, 4], BF16, name="x_grouped", tag="x_grouped", align_bytes=64)
-            banks = []
-            for b in range(B):
-                words = x_raw[j][:, b, :].bitcast(F32)
-                bank = psum.tile([P, 2 * PASSES, P], F32, name="x_bank", tag="bank")
+        def transpose_x(b, i, copies):
+            grouped = x_grouped_pool.tile([P, PASSES, 2, P, 4], BF16, name="x_grouped", tag="x_grouped", align_bytes=64)
+            for jj in range(2):
+                words = x_raw[b][i][:, jj, :].bitcast(F32)
+                bank = t_psum.tile([P, PASSES, 2, P], F32, name="x_bank", tag="t")
                 for g in range(PASSES):
                     for u in range(2):
-                        nc.tensor.transpose(
-                            bank[:, 2 * g + u, :], words[:, 2 * P * g + u:2 * P * (g + 1):2], ident[:]
-                        )
-                banks.append(bank)
-            for b in range(B):
-                nc.scalar.copy(
-                    out=grouped[:].bitcast(F32)[:, b], in_=banks[b][:].rearrange("p (g u) r -> p g r u", u=2)
+                        nc.tensor.transpose(bank[:, g, u, :], words[:, 2 * P * g + u:2 * P * (g + 1):2], ident[:])
+                copies[jj](
+                    out=grouped[:, :, jj].rearrange("p g r t -> p g (r t)").bitcast(F32).rearrange("p g (r u) -> p g r u", u=2),
+                    in_=bank[:].rearrange("p g u r -> p g r u"),
                 )
             return grouped
 
-        def quantise_x(j, grouped):
-            for b in range(B):
-                for g in range(PASSES):
-                    nc.vector.quantize_mx(
-                        out=x_codes[:, b, g, j, :].bitcast(FP8X4),
-                        scales=x_scales[:, b, g, j, :],
-                        in_=grouped[:, b, g].rearrange("p r t -> p (r t)"),
-                    )
+        def quantise_x(b, i, grouped):
+            for g in range(PASSES):
+                nc.vector.quantize_mx(
+                    out=x_codes[:, b, g, 2 * i:2 * i + 2, :].rearrange("p j r -> p (j r)").bitcast(FP8X4),
+                    scales=x_scales[:, b, g, 2 * i:2 * i + 2, :].rearrange("p j r -> p (j r)"),
+                    in_=grouped[:, g].rearrange("p j r t -> p (j r t)"),
+                )
 
         w_grouped = {}
 
-        def regroup_w(copy, pieces, c, g):
-            if g == 0:
-                w_grouped[c] = w_grouped_pool.tile(
+        def grouped_tile(w, part, g):
+            if (w, part) not in w_grouped:
+                pool = v_grouped_pool if w == 2 else w_grouped_pool
+                w_grouped[(w, part)] = pool.tile(
                     [P, PASSES, BANK, 4], BF16, name="w_grouped", tag="w_grouped", align_bytes=64
                 )
-            width = BANK // pieces
-            for i in range(pieces):
-                copy(
-                    out=w_grouped[c][:, g, i * width:(i + 1) * width, :].rearrange("p (c i) t -> p c t i", i=4),
-                    in_=w_raw[c][:, 4 * g:4 * g + 4, i * width:(i + 1) * width].rearrange("p t (c i) -> p c t i", i=4),
-                )
+            return w_grouped[(w, part)][:, g]
 
-        def quantise_w(c):
-            nc.vector.quantize_mx(
-                out=w_codes[c][:].rearrange("p g c -> p (g c)").bitcast(FP8X4),
-                scales=w_scales[c][:].rearrange("p g c -> p (g c)"),
-                in_=w_grouped[c][:].rearrange("p g c t -> p (g c t)"),
+        def regroup_qk(copy, w, part, g, source, first_head, heads):
+            dst = grouped_tile(w, part, g)[:, first_head * R:(first_head + heads) * R, :]
+            src = source.rearrange("p t (h e c i) -> p h e c t i", e=2, c=R // 4, i=4)
+            copy(out=dst.rearrange("p (h c i) t -> p h c t i", c=R // 4, i=4), in_=src[:, :, part])
+
+        def regroup_v(copy, part, g):
+            src = w_raw[2][g][:, :, part * BANK:(part + 1) * BANK]
+            copy(
+                out=grouped_tile(2, part, g).rearrange("p (c i) t -> p c t i", i=4),
+                in_=src.rearrange("p t (c i) -> p c t i", i=4),
             )
 
-        def unit_products(unit):
-            c, j = unit // TILES, unit % TILES
-            head0 = CHUNKS[c][0] * H + CHUNKS[c][1] * HEADS
-            turned_bank = psum.tile([P, HEADS, R], F32, name="turned_bank", tag="bank")
-            nc.tensor.matmul(
-                out=turned_bank[:].rearrange("p h j -> p (h j)"),
-                lhsT=table_T[:, j, :],
-                rhs=bias_masked[:, head0:head0 + HEADS, :].rearrange("p r j -> p (r j)"),
-                start=True,
-                stop=True,
-            )
-            banks = []
-            for b in range(B):
-                bank = psum.tile([P, BANK], F32, name="unit_bank", tag="bank")
-                mx_product(
-                    bank[:],
-                    lambda g: x_codes[:, b, g, j, :],
-                    lambda g: x_scales[:, b, g, j, :],
-                    lambda g: w_codes[c][:, g, :],
-                    lambda g: w_scales[c][:, g, :],
-                )
-                banks.append(bank)
-            turned_bias = turned_bank
-            if not vector_adds_turned_bias(unit):
-                turned_bias = turned_bias_pool.tile([P, HEADS, R], F32, name="turned_bias", tag="turned_bias")
-                nc.scalar.copy(out=turned_bias[:], in_=turned_bank[:])
-            return banks, turned_bias
-
-        def unit_finish(unit, banks, turned_bias):
-            c, j = unit // TILES, unit % TILES
-            which, half = CHUNKS[c]
-            head0 = which * H + half * HEADS
-            products = products_pool.tile([P, B, HEADS, 2, R], F32, name="products", tag="products")
-            result = unit_out_pool.tile([P, B, BANK], F32, name="unit_out", tag="unit_out")
-            for b in range(B):
-                heads = banks[b][:].rearrange("p (h d) -> p h d", d=D)
-                nc.vector.tensor_tensor(
-                    out=products[:, b],
-                    in0=heads[:, :, 0:R].unsqueeze(2).to_broadcast([P, HEADS, 2, R]),
-                    in1=factors[:, j].unsqueeze(1).to_broadcast([P, HEADS, 2, R]),
-                    op=ALU.mult,
-                )
-                nc.vector.tensor_tensor(
-                    out=result[:, b, :].rearrange("p (h d) -> p h d", d=D)[:, :, R:D],
-                    in0=heads[:, :, R:D],
-                    in1=pass_bias[:, head0:head0 + HEADS, :],
-                    op=ALU.add,
-                )
-            for_both = turned_bias[:].unsqueeze(1).to_broadcast([P, B, HEADS, R])
-            if vector_adds_turned_bias(unit):
-                with_cos = products[:, :, :, 0, :]
-                nc.vector.tensor_tensor(out=with_cos, in0=with_cos, in1=for_both, op=ALU.add)
-            heads = result[:].rearrange("p b (h d) -> p (b h) d", d=D)
-            pairs = products[:].rearrange("p b h c j -> p (b h) c j")
-            nc.gpsimd.tensor_tensor(
-                out=heads[:, :, 0:HALF], in0=pairs[:, :, 0, 0:HALF], in1=pairs[:, :, 1, HALF:R], op=ALU.add
-            )
-            nc.gpsimd.tensor_tensor(
-                out=heads[:, :, HALF:R], in0=pairs[:, :, 0, HALF:R], in1=pairs[:, :, 1, 0:HALF], op=ALU.add
-            )
-            if not vector_adds_turned_bias(unit):
-                turned = result[:].rearrange("p b (h d) -> p b h d", d=D)[:, :, :, 0:R]
-                nc.gpsimd.tensor_tensor(out=turned, in0=turned, in1=for_both, op=ALU.add)
-            dst = outs[which].rearrange("b s h d -> s b (h d)")
-            nc.sync.dma_start(out=dst[j * P:(j + 1) * P, :, half * BANK:(half + 1) * BANK], in_=result[:])
-
-        v_T = {}
-        v_out = {}
-
-        def v_front(pair):
-            banks = []
-            for n in (2 * pair, 2 * pair + 1):
-                c, b, f = V_CHUNKS[n // STEPS_PER_CHUNK], (n // FEATURE_TILES) % B, n % FEATURE_TILES
-                bank = psum.tile([P, BANK], F32, name="v_bank", tag="bank")
-                mx_product(
-                    bank[:],
-                    lambda g: w_codes[c][:, g, f * P:(f + 1) * P],
-                    lambda g: w_scales[c][:, g, f * P:(f + 1) * P],
-                    lambda g: x_codes[:, b, g].rearrange("p j r -> p (j r)"),
-                    lambda g: x_scales[:, b, g].rearrange("p j r -> p (j r)"),
-                )
-                banks.append(bank)
-            for n in (2 * pair, 2 * pair + 1):
-                column = CHUNKS[V_CHUNKS[n // STEPS_PER_CHUNK]][1] * FEATURE_TILES + n % FEATURE_TILES
-                v_T[n] = v_T_pool.tile([P, BANK], F32, name="v_T", tag="v_T")
-                nc.scalar.activation(
-                    out=v_T[n][:], in_=banks[n % 2][:], func=ACT.Identity, bias=v_bias[:, column:column + 1], scale=1.0
-                )
-
-        def v_back(pair):
-            banks = []
-            for n in (2 * pair, 2 * pair + 1):
-                bank = psum.tile([P, TILES, P], F32, name="v_back", tag="bank")
-                for j in range(TILES):
-                    nc.tensor.transpose(bank[:, j, :], v_T[n][:, j * P:(j + 1) * P], ident[:])
-                banks.append(bank)
-            for n in (2 * pair, 2 * pair + 1):
-                quarter, f = n // FEATURE_TILES, n % FEATURE_TILES
-                if f == 0:
-                    v_out[quarter] = v_out_pool.tile([P, TILES, BANK], F32, name="v_out", tag="v_out")
-                nc.scalar.copy(out=v_out[quarter][:, :, f * P:(f + 1) * P], in_=banks[n % 2][:])
-                if f == FEATURE_TILES - 1:
-                    half, b = CHUNKS[V_CHUNKS[quarter // B]][1], quarter % B
-                    dst = out_2.rearrange("b (j p) h d -> p b j (h d)", p=P)
-                    nc.sync.dma_start(out=dst[:, b, :, half * BANK:(half + 1) * BANK], in_=v_out[quarter][:])
-
-        table_bank = psum.tile([P, TILES, P], BF16, name="table_bank", tag="bank")
-        for t in range(TILES):
-            nc.tensor.transpose(table_bank[:, t, :], table[:, t, :], ident16[:])
-        bias_bank = psum.tile([P, P], BF16, name="bias_bank", tag="bank")
-        nc.tensor.transpose(bias_bank[:], bias_rows[:], ident16[:])
-        nc.scalar.copy(out=table_T[:], in_=table_bank[:])
-        nc.vector.tensor_tensor(
-            out=bias_masked[:],
-            in0=bias_bank[:, 0:2 * H].unsqueeze(2).to_broadcast([P, 2 * H, R]),
-            in1=mask[:].unsqueeze(1).to_broadcast([P, 2 * H, R]),
-            op=ALU.mult,
-        )
-        nc.vector.tensor_copy(out=v_bias[:], in_=bias_bank[:, 2 * H:2 * H + 2 * FEATURE_TILES])
-        x_grouped = {0: transpose_x(0)}
-        pass_banks = []
-        for w in range(2):
-            pass_bank = psum.tile([P, H, R], F32, name="pass_bank", tag="bank")
-            nc.tensor.matmul(
-                out=pass_bank[:].rearrange("p h j -> p (h j)"),
-                lhsT=selector[:],
-                rhs=bias_masked[:, w * H:(w + 1) * H, :].rearrange("p r j -> p (r j)"),
-                start=True,
-                stop=True,
-            )
-            pass_banks.append(pass_bank)
-        for w in range(2):
-            nc.scalar.copy(out=pass_bias[:, w * H:(w + 1) * H, :], in_=pass_banks[w][:])
-        for g in range(PASSES):
-            regroup_w(nc.vector.tensor_copy, 1, 0, g)
-        quantise_x(0, x_grouped[0])
-        quantise_w(0)
-        x_grouped[1] = transpose_x(1)
-        quantise_x(1, x_grouped[1])
-
-        scalar_passes = [(c, g) for c in (4, 1, 2, 5, 3) for g in range(PASSES)]
-        v_parts = []
-        for pair in range(V_PAIRS + 1):
-            if pair < V_PAIRS:
-                v_parts.append(("front", pair))
-            if pair >= 1:
-                v_parts.append(("back", pair - 1))
-        quantise_after = {3: (4, 1), 6: (2,), 8: (5,), 10: (3,)}
-        placed = 0
-        for unit in range(UNITS):
-            banks, turned_bias = unit_products(unit)
-            if unit == 1:
-                for j in (2, 3):
-                    x_grouped[j] = transpose_x(j)
-            for i in range((1, 1, 2, 2)[unit] if unit < 4 else 0):
-                regroup_w(nc.scalar.copy, 2, scalar_passes[0][0], scalar_passes[0][1])
-                scalar_passes = scalar_passes[1:]
-            while placed < min(len(v_parts), (3 * (unit - 4) + 1) // 2):
-                part, pair = v_parts[placed]
-                if part == "front":
-                    v_front(pair)
+        def regroup_on_gpsimd(w, part, g, source, first, count, pieces):
+            width = count // pieces
+            for c0 in range(first, first + count, width):
+                dst = grouped_tile(w, part, g)[:, c0:c0 + width, :]
+                if w == 2:
+                    src = source[:, :, c0 - first:c0 - first + width].rearrange("p t c -> p c t")
                 else:
-                    v_back(pair)
-                if scalar_passes and placed % 2 == 0:
-                    regroup_w(nc.scalar.copy, 2, scalar_passes[0][0], scalar_passes[0][1])
-                    scalar_passes = scalar_passes[1:]
-                placed += 1
-            unit_finish(unit, banks, turned_bias)
-            if unit == 1:
-                for j in (2, 3):
-                    quantise_x(j, x_grouped[j])
-            for c in quantise_after.get(unit, ()):
-                quantise_w(c)
+                    src = heads_of_rows(source, (c0 - first) // R, width // R, part)
+                    dst = dst.rearrange("p (h j) t -> p h j t", j=R)
+                nc.gpsimd.tensor_scalar(out=dst, in0=src, scalar1=1.0, scalar2=0.0, op0=ALU.mult, op1=ALU.add)
+
+        def heads_of_rows(source, first_head, heads, part):
+            rows = source.rearrange("p t (h e j) -> p h e j t", e=2, j=R)
+            return rows[:, first_head:first_head + heads, part]
+
+        def quantise_w(w, part):
+            nc.vector.quantize_mx(
+                out=w_codes[w][part][:].rearrange("p g c -> p (g c)").bitcast(FP8X4),
+                scales=w_scales[w][part][:].rearrange("p g c -> p (g c)"),
+                in_=w_grouped[(w, part)][:].rearrange("p g c t -> p (g c t)"),
+            )
+
+        def quantise_half(w, part, g, half):
+            c0 = half * HG * R
+            nc.vector.quantize_mx(
+                out=w_codes[w][part][:, g, c0:c0 + HG * R].bitcast(FP8X4),
+                scales=w_scales[w][part][:, g, c0:c0 + HG * R],
+                in_=w_grouped[(w, part)][:, g, c0:c0 + HG * R, :].rearrange("p c t -> p (c t)"),
+            )
+
+        y = {}
+
+        def turned_product(block, f, direct=True):
+            w, b = BLOCKS[block]
+            bank = a_psum.tile([P, BANK], F32, name="a_bank", tag="a")
+            mx_product(
+                bank[:],
+                lambda g: w_codes[w][0][:, g, f * P:(f + 1) * P],
+                lambda g: w_scales[w][0][:, g, f * P:(f + 1) * P],
+                lambda g: x_codes[:, b, g].rearrange("p j r -> p (j r)"),
+                lambda g: x_scales[:, b, g].rearrange("p j r -> p (j r)"),
+            )
+            y[(block, f)] = y_pool.tile([P, 2, BANK], F32, name="y", tag="y")
+            if not direct:
+                biased = biased_pool.tile([P, BANK], F32, name="biased", tag="biased")
+                nc.scalar.activation(
+                    out=biased[:], in_=bank[:], func=ACT.Identity, bias=turned_bias[:, FT * w + f:FT * w + f + 1], scale=1.0
+                )
+                for c in (1, 0):
+                    nc.gpsimd.tensor_tensor(out=y[(block, f)][:, c], in0=biased[:], in1=table_T[:, c], op=ALU.mult)
+                return
+            nc.vector.scalar_tensor_tensor(
+                out=y[(block, f)][:],
+                in0=bank[:].unsqueeze(1).to_broadcast([P, 2, BANK]),
+                scalar=turned_bias[:, FT * w + f:FT * w + f + 1],
+                in1=table_T[:],
+                op0=ALU.add,
+                op1=ALU.mult,
+            )
+
+        result = {}
+
+        def result_tile(w, b, i):
+            if (w, b, i) not in result:
+                result[(w, b, i)] = result_pool.tile([P, 2, E], F32, name="result", tag="result")
+            return result[(w, b, i)]
+
+        def heads_of(tile_row, lo, hi):
+            return tile_row.rearrange("p (h d) -> p h d", d=D)[:, :, lo:hi]
+
+        def turned_back(block, j):
+            w, b = BLOCKS[block]
+            bank = t_psum.tile([P, FT, P], F32, name="t_bank", tag="t")
+            for f in range(FT):
+                for c, permutation in ((0, ident), (1, swap)):
+                    nc.tensor.matmul(
+                        out=bank[:, f, :],
+                        lhsT=y[(block, f)][:, c, j * P:(j + 1) * P],
+                        rhs=permutation[:],
+                        is_transpose=True,
+                        start=(c == 0),
+                        stop=(c == 1),
+                    )
+            nc.scalar.copy(
+                out=heads_of(result_tile(w, b, j // 2)[:, j % 2, :], 0, R),
+                in_=bank[:].rearrange("p f (h j) -> p (f h) j", j=R),
+            )
+
+        def store(w, b, i):
+            dst = outs[w][b].rearrange("(p t) h d -> p t (h d)", t=TILES)
+            nc.sync.dma_start(out=dst[:, 2 * i:2 * i + 2, :], in_=result[(w, b, i)][:])
+
+        def add_bias(out, product, bias, direct):
+            if direct:
+                nc.vector.tensor_tensor(out=out, in0=product, in1=bias, op=ALU.add)
+            else:
+                nc.scalar.copy(out=out, in_=product)
+                nc.gpsimd.tensor_tensor(out=out, in0=out, in1=bias, op=ALU.add)
+
+        def store_row(w, b, j):
+            dst = outs[w][b].rearrange("(p t) h d -> p t (h d)", t=TILES)
+            nc.sync.dma_start(out=dst[:, j:j + 1, :], in_=result[(w, b, j // 2)][:, j % 2:j % 2 + 1, :])
+
+        def row_product(w, part, b, j):
+            bank = p_psum.tile([P, BANK], F32, name="p_bank", tag="p")
+            mx_product(
+                bank[:],
+                lambda g: x_codes[:, b, g, j, :],
+                lambda g: x_scales[:, b, g, j, :],
+                lambda g: w_codes[w][part][:, g, :],
+                lambda g: w_scales[w][part][:, g, :],
+            )
+            return bank
+
+        def passing(block, j, direct=True):
+            w, b = BLOCKS[block]
+            bank = row_product(w, 1, b, j)
+            out = heads_of(result_tile(w, b, j // 2)[:, j % 2, :], R, D)
+            product = bank[:].rearrange("p (h j) -> p h j", j=R)
+            bias = pass_bias[:, w, :].rearrange("p (h j) -> p h j", j=R)
+            add_bias(out, product, bias, direct)
+
+        def v_unit(b, j, half, direct):
+            bank = row_product(2, half, b, j)
+            out = result_tile(2, b, j // 2)[:, j % 2, half * BANK:(half + 1) * BANK]
+            bias = v_bias[:, half * BANK:(half + 1) * BANK]
+            add_bias(out, bank[:], bias, direct)
+
+        nc.vector.tensor_copy(out=ident16[:], in_=ident[:])
+        for lo, hi in ((0, HALF), (HALF, R)):
+            blocks_out = swap[:].rearrange("p (h j) -> p h j", j=R)
+            blocks_in = ident[:].rearrange("p (h j) -> p h j", j=R)
+            nc.vector.tensor_copy(out=blocks_out[:, :, lo:hi], in_=blocks_in[:, :, HALF - lo:HALF - lo + HALF])
+
+        def make_tables():
+            nc.vector.tensor_copy(out=table[:, 0], in_=cos16[:].unsqueeze(2).to_broadcast([P, TILES, 4, R]))
+            nc.vector.tensor_copy(
+                out=table[:, 1, :, :, 0:HALF], in_=sin16[:, :, HALF:R].unsqueeze(2).to_broadcast([P, TILES, 4, HALF])
+            )
+            nc.vector.tensor_scalar_mul(
+                out=table[:, 1, :, :, HALF:R],
+                in0=sin16[:, :, 0:HALF].unsqueeze(2).to_broadcast([P, TILES, 4, HALF]),
+                scalar1=-1.0,
+            )
+            table_bank = a_psum.tile([P, 2, TILES, P], BF16, name="table_bank", tag="a")
+            for c in range(2):
+                for j in range(TILES):
+                    nc.tensor.transpose(
+                        table_bank[:, c, j, :], table[:, c, j].rearrange("p h j -> p (h j)"), ident16[:]
+                    )
+            nc.scalar.copy(out=table_T[:], in_=table_bank[:].rearrange("p c j r -> p c (j r)"))
+            rows_bank = a_psum.tile([P, P], BF16, name="rows_bank", tag="a")
+            nc.tensor.transpose(rows_bank[:], turned_rows[:], ident16[:])
+            nc.vector.tensor_copy(out=turned_bias[:], in_=rows_bank[:, 0:2 * FT])
+
+        def spread_bias(copy_out, sources):
+            bank = p_psum.tile([P, 2, BANK], BF16, name="bias_bank", tag="p")
+            for i in range(2):
+                nc.tensor.matmul(
+                    out=bank[:, i, :].rearrange("p (h j) -> p h j", j=R), lhsT=ones[:], rhs=sources[i], start=True, stop=True
+                )
+            nc.scalar.copy(out=copy_out, in_=bank[:].rearrange("p i c -> p (i c)"))
+
+        def finish(block, i):
+            w, b = BLOCKS[block]
+            for j in (2 * i, 2 * i + 1):
+                turned_back(block, j)
+            store(w, b, i)
+
+        scalar_only = (nc.scalar.copy, nc.scalar.copy)
+        both = (nc.scalar.copy, nc.vector.tensor_copy)
+        v, s = nc.vector.tensor_copy, nc.scalar.copy
+        x_grouped = {}
+        make_tables()
+        x_grouped[(0, 0)] = transpose_x(0, 0, both)
+        regroup_qk(v, 0, 0, 0, wq_raw[0][0][:], 0, HG)
+        quantise_x(0, 0, x_grouped[(0, 0)])
+        spread_bias(
+            pass_bias[:].rearrange("p w c -> p (w c)"),
+            [heads_of(bias_row[:, w * E:(w + 1) * E], R, D) for w in range(2)],
+        )
+        quantise_half(0, 0, 0, 0)
+        x_grouped[(0, 1)] = transpose_x(0, 1, scalar_only)
+        regroup_qk(v, 0, 0, 1, wq_raw[0][1][:], 0, HG)
+        quantise_x(0, 1, x_grouped[(0, 1)])
+        quantise_half(0, 0, 1, 0)
+        for g in range(PASSES):
+            regroup_qk(s, 0, 1, g, wq_raw[0][g][:], 0, HG)
+
+        turned_product(0, 0)
+        turned_product(0, 1)
+        for g in range(PASSES):
+            regroup_qk(v if g else s, 0, 0, g, wq_raw[1][g][:], HG, HG)
+        for g in range(PASSES):
+            regroup_on_gpsimd(0, 1, g, wq_raw[1][g][:], HG * R, HG * R, 2)
+        x_grouped[(1, 0)] = transpose_x(1, 0, scalar_only)
+        x_grouped[(1, 1)] = transpose_x(1, 1, scalar_only)
+        for g in range(PASSES):
+            quantise_half(0, 0, g, 1)
+        turned_product(0, 2)
+        turned_product(0, 3)
+        quantise_w(0, 1)
+        passing(0, 0)
+        passing(0, 1)
+        quantise_x(1, 0, x_grouped[(1, 0)])
+        quantise_x(1, 1, x_grouped[(1, 1)])
+        regroup_qk(s, 1, 0, 0, w_raw[1][0][:], 0, H)
+        finish(0, 0)
+        for g in range(PASSES):
+            regroup_on_gpsimd(1, 1, g, w_raw[1][g][:], 0, BANK, 4)
+        passing(0, 2)
+        passing(0, 3)
+        regroup_qk(s, 1, 0, 1, w_raw[1][1][:], 0, H)
+        for part in range(2):
+            for g in range(PASSES):
+                if part == 0:
+                  regroup_on_gpsimd(2, part, g, w_raw[2][g][:, :, part * BANK:(part + 1) * BANK], 0, BANK, 4)
+
+        for block in range(1, 4):
+            turned_product(block, 0)
+            turned_product(block, 1)
+            finish(block - 1, 1)
+            turned_product(block, 2)
+            turned_product(block, 3)
+            if block == 1:
+                quantise_w(1, 0)
+            passing(block, 0)
+            passing(block, 1)
+            finish(block, 0)
+            passing(block, 2)
+            passing(block, 3)
+            if block == 1:
+                regroup_v(s, 1, 0)
+                regroup_v(s, 1, 1)
+                spread_bias(v_bias[:], [
+                    bias_row[:, 2 * E + half * BANK:2 * E + (half + 1) * BANK].rearrange("p (h j) -> p h j", j=R)
+                    for half in range(2)
+                ])
+                quantise_w(1, 1)
+            if block == 2:
+                quantise_w(2, 0)
+            if block == 3:
+                quantise_w(2, 1)
+
+        finish(3, 1)
+        for b in range(B):
+            for j in range(TILES):
+                last = b == B - 1 and j == TILES - 1
+                for half in range(2):
+                    v_unit(b, j, half, half == 0 or last)
+                store_row(2, b, j)

@@ -32,14 +32,14 @@ def tile_improvedattention_pa_kernel(tc, x, W_qkv, b_qkv, sin_tab, cos_tab, out_
         ctx.enter_context(tc.manual_schedule())
         keep = ctx.enter_context(tc.tile_pool(name="keep", bufs=1))
         x_grouped_pool = ctx.enter_context(tc.tile_pool(name="x_grouped", bufs=2))
-        w_grouped_pool = ctx.enter_context(tc.tile_pool(name="w_grouped", bufs=2))
+        w_grouped_pool = ctx.enter_context(tc.tile_pool(name="w_grouped", bufs=3))
         v_grouped_pool = ctx.enter_context(tc.tile_pool(name="v_grouped", bufs=2))
         y_pool = ctx.enter_context(tc.tile_pool(name="y", bufs=10))
         biased_pool = ctx.enter_context(tc.tile_pool(name="biased", bufs=2))
         result_pool = ctx.enter_context(tc.tile_pool(name="result", bufs=7))
-        a_psum = ctx.enter_context(tc.psum_pool(name="a_psum", bufs=3))
+        a_psum = ctx.enter_context(tc.psum_pool(name="a_psum", bufs=2))
         t_psum = ctx.enter_context(tc.psum_pool(name="t_psum", bufs=2))
-        p_psum = ctx.enter_context(tc.psum_pool(name="p_psum", bufs=3))
+        p_psum = ctx.enter_context(tc.psum_pool(name="p_psum", bufs=4))
 
         x_raw = [[y_pool.tile([P, 2, E], BF16, name="x_raw", tag="y") for i in range(2)] for b in range(B)]
         wq_raw = [[y_pool.tile([P, 4, BANK], BF16, name="wq_raw", tag="y") for g in range(PASSES)] for i in range(2)]
@@ -58,8 +58,7 @@ def tile_improvedattention_pa_kernel(tc, x, W_qkv, b_qkv, sin_tab, cos_tab, out_
         sin16 = keep.tile([P, TILES, R], BF16)
         table = keep.tile([P, 2, TILES, 4, R], BF16)
         table_T = keep.tile([P, 2, BANK], BF16)
-        bias_row = keep.tile([P, 3 * E], BF16)
-        ones = keep.tile([P, P], BF16)
+        bias_rows = keep.tile([P, P], BF16)
         turned_rows = keep.tile([P, P], BF16)
         turned_bias = keep.tile([P, 2 * FT], F32)
         pass_bias = keep.tile([P, 2, BANK], BF16)
@@ -68,17 +67,9 @@ def tile_improvedattention_pa_kernel(tc, x, W_qkv, b_qkv, sin_tab, cos_tab, out_
         ident16 = keep.tile([P, P], BF16)
         swap = keep.tile([P, P], F32)
 
-        make_identity(nc, ident[:])
         nc.vector.memset(turned_rows[:], 0.0)
-        nc.vector.memset(ones[:], 1.0)
-        nc.gpsimd.memset(bias_row[:].bitcast(U32), 0)
-        nc.scalar.dma_start(out=cos16[:], in_=cos_tab.rearrange("(p t) j -> p t j", t=TILES))
-        nc.scalar.dma_start(out=sin16[:], in_=sin_tab.rearrange("(p t) j -> p t j", t=TILES))
-        nc.scalar.dma_start(
-            out=turned_rows[0:2 * FT, :].rearrange("r (h j) -> r h j", j=R),
-            in_=b_qkv[0:2 * E].rearrange("(r h d) -> r h d", h=4, d=D)[:, :, 0:R],
-        )
-        nc.scalar.dma_start(out=bias_row[0:1, :], in_=b_qkv.rearrange("(o c) -> o c", o=1))
+        nc.vector.memset(bias_rows[:], 0.0)
+        make_identity(nc, ident[:])
 
         def load_x(b, i):
             src = x[b].rearrange("(p t) k -> p t k", t=TILES)
@@ -91,6 +82,13 @@ def tile_improvedattention_pa_kernel(tc, x, W_qkv, b_qkv, sin_tab, cos_tab, out_
         load_x(0, 0)
         load_wq(0, 0)
         load_x(0, 1)
+        nc.sync.dma_start(out=cos16[:], in_=cos_tab.rearrange("(p t) j -> p t j", t=TILES))
+        nc.sync.dma_start(out=sin16[:], in_=sin_tab.rearrange("(p t) j -> p t j", t=TILES))
+        nc.sync.dma_start(
+            out=turned_rows[0:2 * FT, :].rearrange("r (h j) -> r h j", j=R),
+            in_=b_qkv[0:2 * E].rearrange("(r h d) -> r h d", h=4, d=D)[:, :, 0:R],
+        )
+        nc.sync.dma_start(out=bias_rows[0:3 * E // P, :], in_=b_qkv.rearrange("(r c) -> r c", c=P))
         load_wq(0, 1)
         load_wq(1, 0)
         load_wq(1, 1)
@@ -312,13 +310,17 @@ def tile_improvedattention_pa_kernel(tc, x, W_qkv, b_qkv, sin_tab, cos_tab, out_
             nc.tensor.transpose(rows_bank[:], turned_rows[:], ident16[:])
             nc.vector.tensor_copy(out=turned_bias[:], in_=rows_bank[:, 0:2 * FT])
 
-        def spread_bias(copy_out, sources):
-            bank = p_psum.tile([P, 2, BANK], BF16, name="bias_bank", tag="p")
-            for i in range(2):
+        def spread_rows(rows, lo, hi, copy_out):
+            bank = p_psum.tile([P, 2 * len(rows), hi - lo], BF16, name="bias_bank", tag="p")
+            for i, r in enumerate(rows):
                 nc.tensor.matmul(
-                    out=bank[:, i, :].rearrange("p (h j) -> p h j", j=R), lhsT=ones[:], rhs=sources[i], start=True, stop=True
+                    out=bank[:, 2 * i:2 * i + 2, :],
+                    lhsT=ident16[:, r:r + 1].to_broadcast([P, P]),
+                    rhs=heads_of(bias_rows[:], lo, hi),
+                    start=True,
+                    stop=True,
                 )
-            nc.scalar.copy(out=copy_out, in_=bank[:].rearrange("p i c -> p (i c)"))
+            nc.scalar.copy(out=copy_out, in_=bank[:].rearrange("p h j -> p (h j)"))
 
         def finish(block, i):
             w, b = BLOCKS[block]
@@ -326,54 +328,44 @@ def tile_improvedattention_pa_kernel(tc, x, W_qkv, b_qkv, sin_tab, cos_tab, out_
                 turned_back(block, j)
             store(w, b, i)
 
-        scalar_only = (nc.scalar.copy, nc.scalar.copy)
-        both = (nc.scalar.copy, nc.vector.tensor_copy)
         v, s = nc.vector.tensor_copy, nc.scalar.copy
         x_grouped = {}
-        make_tables()
-        x_grouped[(0, 0)] = transpose_x(0, 0, both)
+        x_grouped[(0, 0)] = transpose_x(0, 0, (s, v))
         regroup_qk(v, 0, 0, 0, wq_raw[0][0][:], 0, HG)
         quantise_x(0, 0, x_grouped[(0, 0)])
-        spread_bias(
-            pass_bias[:].rearrange("p w c -> p (w c)"),
-            [heads_of(bias_row[:, w * E:(w + 1) * E], R, D) for w in range(2)],
-        )
+        x_grouped[(0, 1)] = transpose_x(0, 1, (s, s))
+        make_tables()
+        regroup_qk(s, 0, 1, 0, wq_raw[0][0][:], 0, HG)
         quantise_half(0, 0, 0, 0)
-        x_grouped[(0, 1)] = transpose_x(0, 1, scalar_only)
         regroup_qk(v, 0, 0, 1, wq_raw[0][1][:], 0, HG)
         quantise_x(0, 1, x_grouped[(0, 1)])
         quantise_half(0, 0, 1, 0)
-        for g in range(PASSES):
-            regroup_qk(s, 0, 1, g, wq_raw[0][g][:], 0, HG)
+        spread_rows(range(0, 16), R, D, pass_bias[:].rearrange("p w c -> p (w c)"))
+        regroup_qk(s, 0, 1, 1, wq_raw[0][1][:], 0, HG)
 
         turned_product(0, 0)
         turned_product(0, 1)
         for g in range(PASSES):
             regroup_qk(v if g else s, 0, 0, g, wq_raw[1][g][:], HG, HG)
         for g in range(PASSES):
-            regroup_on_gpsimd(0, 1, g, wq_raw[1][g][:], HG * R, HG * R, 2)
-        x_grouped[(1, 0)] = transpose_x(1, 0, scalar_only)
-        x_grouped[(1, 1)] = transpose_x(1, 1, scalar_only)
-        for g in range(PASSES):
             quantise_half(0, 0, g, 1)
+        x_grouped[(1, 0)] = transpose_x(1, 0, (s, s))
         turned_product(0, 2)
         turned_product(0, 3)
+        for g in range(PASSES):
+            regroup_qk(v if g else s, 0, 1, g, wq_raw[1][g][:], HG, HG)
+        x_grouped[(1, 1)] = transpose_x(1, 1, (s, v))
         quantise_w(0, 1)
-        passing(0, 0)
-        passing(0, 1)
         quantise_x(1, 0, x_grouped[(1, 0)])
+        for j in range(TILES):
+            passing(0, j)
         quantise_x(1, 1, x_grouped[(1, 1)])
-        regroup_qk(s, 1, 0, 0, w_raw[1][0][:], 0, H)
+        for g in range(PASSES):
+            regroup_qk(s, 1, 0, g, w_raw[1][g][:], 0, H)
         finish(0, 0)
         for g in range(PASSES):
-            regroup_on_gpsimd(1, 1, g, w_raw[1][g][:], 0, BANK, 4)
-        passing(0, 2)
-        passing(0, 3)
-        regroup_qk(s, 1, 0, 1, w_raw[1][1][:], 0, H)
-        for part in range(2):
-            for g in range(PASSES):
-                if part == 0:
-                  regroup_on_gpsimd(2, part, g, w_raw[2][g][:, :, part * BANK:(part + 1) * BANK], 0, BANK, 4)
+            regroup_qk(s, 1, 1, g, w_raw[1][g][:], 0, H)
+        spread_rows(range(16, 24), 0, D, v_bias[:])
 
         for block in range(1, 4):
             turned_product(block, 0)
@@ -385,17 +377,15 @@ def tile_improvedattention_pa_kernel(tc, x, W_qkv, b_qkv, sin_tab, cos_tab, out_
                 quantise_w(1, 0)
             passing(block, 0)
             passing(block, 1)
-            finish(block, 0)
             passing(block, 2)
             passing(block, 3)
+            finish(block, 0)
             if block == 1:
-                regroup_v(s, 1, 0)
-                regroup_v(s, 1, 1)
-                spread_bias(v_bias[:], [
-                    bias_row[:, 2 * E + half * BANK:2 * E + (half + 1) * BANK].rearrange("p (h j) -> p h j", j=R)
-                    for half in range(2)
-                ])
+                for g in range(PASSES):
+                    regroup_v(v, 0, g)
                 quantise_w(1, 1)
+                for g in range(PASSES):
+                    regroup_v(s, 1, g)
             if block == 2:
                 quantise_w(2, 0)
             if block == 3:

@@ -29,7 +29,6 @@ def tile_improvedattention_pa_kernel(tc, x, W_qkv, b_qkv, sin_tab, cos_tab, out_
     nc = tc.nc
     outs = (out_0, out_1, out_2)
     with ExitStack() as ctx:
-        ctx.enter_context(tc.manual_schedule())
         keep = ctx.enter_context(tc.tile_pool(name="keep", bufs=1))
         x_grouped_pool = ctx.enter_context(tc.tile_pool(name="x_grouped", bufs=2))
         w_grouped_pool = ctx.enter_context(tc.tile_pool(name="w_grouped", bufs=3))
@@ -79,11 +78,11 @@ def tile_improvedattention_pa_kernel(tc, x, W_qkv, b_qkv, sin_tab, cos_tab, out_
             src = W_qkv[4 * P * g:4 * P * (g + 1), i * BANK:(i + 1) * BANK]
             nc.sync.dma_start(out=wq_raw[i][g][:], in_=src.rearrange("(p t) c -> p t c", t=4))
 
+        nc.sync.dma_start(out=cos16[:], in_=cos_tab.rearrange("(p t) j -> p t j", t=TILES))
+        nc.sync.dma_start(out=sin16[:], in_=sin_tab.rearrange("(p t) j -> p t j", t=TILES))
         load_x(0, 0)
         load_wq(0, 0)
         load_x(0, 1)
-        nc.sync.dma_start(out=cos16[:], in_=cos_tab.rearrange("(p t) j -> p t j", t=TILES))
-        nc.sync.dma_start(out=sin16[:], in_=sin_tab.rearrange("(p t) j -> p t j", t=TILES))
         nc.sync.dma_start(
             out=turned_rows[0:2 * FT, :].rearrange("r (h j) -> r h j", j=R),
             in_=b_qkv[0:2 * E].rearrange("(r h d) -> r h d", h=4, d=D)[:, :, 0:R],
@@ -94,7 +93,7 @@ def tile_improvedattention_pa_kernel(tc, x, W_qkv, b_qkv, sin_tab, cos_tab, out_
         load_wq(1, 1)
         load_x(1, 0)
         load_x(1, 1)
-        for w in (1, 2):
+        for w in (2, 1):
             for g in range(PASSES):
                 src = W_qkv[4 * P * g:4 * P * (g + 1), w * E:(w + 1) * E]
                 nc.sync.dma_start(out=w_raw[w][g][:], in_=src.rearrange("(p t) c -> p t c", t=4))
@@ -115,7 +114,7 @@ def tile_improvedattention_pa_kernel(tc, x, W_qkv, b_qkv, sin_tab, cos_tab, out_
             grouped = x_grouped_pool.tile([P, PASSES, 2, P, 4], BF16, name="x_grouped", tag="x_grouped", align_bytes=64)
             for jj in range(2):
                 words = x_raw[b][i][:, jj, :].bitcast(F32)
-                bank = t_psum.tile([P, PASSES, 2, P], F32, name="x_bank", tag="t")
+                bank = p_psum.tile([P, PASSES, 2, P], F32, name="x_bank", tag="p")
                 for g in range(PASSES):
                     for u in range(2):
                         nc.tensor.transpose(bank[:, g, u, :], words[:, 2 * P * g + u:2 * P * (g + 1):2], ident[:])
@@ -306,6 +305,8 @@ def tile_improvedattention_pa_kernel(tc, x, W_qkv, b_qkv, sin_tab, cos_tab, out_
                         table_bank[:, c, j, :], table[:, c, j].rearrange("p h j -> p (h j)"), ident16[:]
                     )
             nc.scalar.copy(out=table_T[:], in_=table_bank[:].rearrange("p c j r -> p c (j r)"))
+
+        def make_turned_bias():
             rows_bank = a_psum.tile([P, P], BF16, name="rows_bank", tag="a")
             nc.tensor.transpose(rows_bank[:], turned_rows[:], ident16[:])
             nc.vector.tensor_copy(out=turned_bias[:], in_=rows_bank[:, 0:2 * FT])
@@ -322,79 +323,131 @@ def tile_improvedattention_pa_kernel(tc, x, W_qkv, b_qkv, sin_tab, cos_tab, out_
                 )
             nc.scalar.copy(out=copy_out, in_=bank[:].rearrange("p h j -> p (h j)"))
 
-        def finish(block, i):
+        def finish(block, i, complete=True):
             w, b = BLOCKS[block]
             for j in (2 * i, 2 * i + 1):
                 turned_back(block, j)
-            store(w, b, i)
+            if complete:
+                store(w, b, i)
 
         v, s = nc.vector.tensor_copy, nc.scalar.copy
         x_grouped = {}
+        make_tables()
         x_grouped[(0, 0)] = transpose_x(0, 0, (s, v))
         regroup_qk(v, 0, 0, 0, wq_raw[0][0][:], 0, HG)
         quantise_x(0, 0, x_grouped[(0, 0)])
         x_grouped[(0, 1)] = transpose_x(0, 1, (s, s))
-        make_tables()
-        regroup_qk(s, 0, 1, 0, wq_raw[0][0][:], 0, HG)
+        make_turned_bias()
         quantise_half(0, 0, 0, 0)
         regroup_qk(v, 0, 0, 1, wq_raw[0][1][:], 0, HG)
         quantise_x(0, 1, x_grouped[(0, 1)])
         quantise_half(0, 0, 1, 0)
-        spread_rows(range(0, 16), R, D, pass_bias[:].rearrange("p w c -> p (w c)"))
-        regroup_qk(s, 0, 1, 1, wq_raw[0][1][:], 0, HG)
-
         turned_product(0, 0)
         turned_product(0, 1)
-        for g in range(PASSES):
-            regroup_qk(v if g else s, 0, 0, g, wq_raw[1][g][:], HG, HG)
-        for g in range(PASSES):
-            quantise_half(0, 0, g, 1)
-        x_grouped[(1, 0)] = transpose_x(1, 0, (s, s))
+        regroup_qk(s, 0, 1, 0, wq_raw[0][0][:], 0 * HG, HG)
+        regroup_qk(s, 0, 1, 1, wq_raw[0][1][:], 0 * HG, HG)
+        regroup_qk(s, 0, 0, 0, wq_raw[1][0][:], HG, HG)
+        regroup_qk(v, 0, 0, 1, wq_raw[1][1][:], HG, HG)
+        quantise_half(0, 0, 0, 1)
+        quantise_half(0, 0, 1, 1)
         turned_product(0, 2)
         turned_product(0, 3)
-        for g in range(PASSES):
-            regroup_qk(v if g else s, 0, 1, g, wq_raw[1][g][:], HG, HG)
-        x_grouped[(1, 1)] = transpose_x(1, 1, (s, v))
-        quantise_w(0, 1)
+        spread_rows(range(0, 16), R, D, pass_bias[:].rearrange("p w c -> p (w c)"))
+        x_grouped[(1, 0)] = transpose_x(1, 0, (s, s))
+        x_grouped[(1, 1)] = transpose_x(1, 1, (s, s))
         quantise_x(1, 0, x_grouped[(1, 0)])
-        for j in range(TILES):
-            passing(0, j)
         quantise_x(1, 1, x_grouped[(1, 1)])
-        for g in range(PASSES):
-            regroup_qk(s, 1, 0, g, w_raw[1][g][:], 0, H)
-        finish(0, 0)
-        for g in range(PASSES):
-            regroup_qk(s, 1, 1, g, w_raw[1][g][:], 0, H)
+        regroup_qk(s, 0, 1, 0, wq_raw[1][0][:], 1 * HG, HG)
+        regroup_qk(v, 0, 1, 1, wq_raw[1][1][:], 1 * HG, HG)
+        quantise_w(0, 1)
+        turned_back(0, 0)
+        turned_back(0, 1)
+        turned_product(1, 0)
+        turned_product(1, 1)
+        passing(0, 0)
+        passing(0, 1)
+        store(*BLOCKS[0], 0)
+        turned_back(0, 2)
+        turned_back(0, 3)
+        turned_product(1, 2)
+        turned_product(1, 3)
+        passing(0, 2)
+        passing(0, 3)
+        store(*BLOCKS[0], 1)
+        passing(1, 0)
+        passing(1, 1)
+        passing(1, 2)
+        passing(1, 3)
+        turned_back(1, 0)
+        turned_back(1, 1)
+        store(*BLOCKS[1], 0)
+        turned_back(1, 2)
+        turned_back(1, 3)
+        store(*BLOCKS[1], 1)
+        regroup_v(v, 0, 0)
+        regroup_v(s, 0, 1)
+        quantise_w(2, 0)
+        regroup_v(s, 1, 0)
+        regroup_v(s, 1, 1)
+        quantise_w(2, 1)
         spread_rows(range(16, 24), 0, D, v_bias[:])
-
-        for block in range(1, 4):
-            turned_product(block, 0)
-            turned_product(block, 1)
-            finish(block - 1, 1)
-            turned_product(block, 2)
-            turned_product(block, 3)
-            if block == 1:
-                quantise_w(1, 0)
-            passing(block, 0)
-            passing(block, 1)
-            passing(block, 2)
-            passing(block, 3)
-            finish(block, 0)
-            if block == 1:
-                for g in range(PASSES):
-                    regroup_v(v, 0, g)
-                quantise_w(1, 1)
-                for g in range(PASSES):
-                    regroup_v(s, 1, g)
-            if block == 2:
-                quantise_w(2, 0)
-            if block == 3:
-                quantise_w(2, 1)
-
-        finish(3, 1)
-        for b in range(B):
-            for j in range(TILES):
-                last = b == B - 1 and j == TILES - 1
-                for half in range(2):
-                    v_unit(b, j, half, half == 0 or last)
-                store_row(2, b, j)
+        v_unit(0, 0, 0, True)
+        v_unit(0, 0, 1, False)
+        store_row(2, 0, 0)
+        v_unit(0, 1, 0, True)
+        v_unit(0, 1, 1, False)
+        store_row(2, 0, 1)
+        regroup_qk(s, 1, 0, 0, w_raw[1][0][:], 0, H)
+        regroup_qk(s, 1, 0, 1, w_raw[1][1][:], 0, H)
+        quantise_w(1, 0)
+        regroup_qk(s, 1, 1, 0, w_raw[1][0][:], 0, H)
+        regroup_qk(s, 1, 1, 1, w_raw[1][1][:], 0, H)
+        quantise_w(1, 1)
+        turned_product(2, 0)
+        turned_product(2, 1)
+        turned_product(2, 2)
+        turned_product(2, 3)
+        v_unit(0, 2, 0, True)
+        v_unit(0, 2, 1, False)
+        store_row(2, 0, 2)
+        v_unit(0, 3, 0, True)
+        v_unit(0, 3, 1, False)
+        store_row(2, 0, 3)
+        passing(2, 0)
+        passing(2, 1)
+        passing(2, 2)
+        passing(2, 3)
+        turned_back(2, 0)
+        turned_back(2, 1)
+        store(*BLOCKS[2], 0)
+        turned_back(2, 2)
+        turned_back(2, 3)
+        store(*BLOCKS[2], 1)
+        turned_product(3, 0)
+        turned_product(3, 1)
+        v_unit(1, 0, 0, True)
+        v_unit(1, 0, 1, False)
+        store_row(2, 1, 0)
+        turned_product(3, 2)
+        turned_product(3, 3)
+        v_unit(1, 1, 0, True)
+        v_unit(1, 1, 1, False)
+        store_row(2, 1, 1)
+        passing(3, 0)
+        passing(3, 1)
+        passing(3, 2)
+        passing(3, 3)
+        v_unit(1, 2, 0, True)
+        v_unit(1, 2, 1, False)
+        store_row(2, 1, 2)
+        turned_back(3, 0)
+        store_row(*BLOCKS[3], 0)
+        turned_back(3, 1)
+        store_row(*BLOCKS[3], 1)
+        v_unit(1, 3, 0, True)
+        v_unit(1, 3, 1, True)
+        store_row(2, 1, 3)
+        turned_back(3, 2)
+        store_row(*BLOCKS[3], 2)
+        turned_back(3, 3)
+        store_row(*BLOCKS[3], 3)

@@ -69,6 +69,7 @@ def tile_improvedattention_pa_kernel(tc, x, W_qkv, b_qkv, sin_tab, cos_tab, out_
         nc.vector.memset(turned_rows[:], 0.0)
         nc.vector.memset(bias_rows[:], 0.0)
         make_identity(nc, ident[:])
+        make_identity(nc, ident16[:])
 
         def load_x(b, i):
             src = x[b].rearrange("(p t) k -> p t k", t=TILES)
@@ -214,6 +215,26 @@ def tile_improvedattention_pa_kernel(tc, x, W_qkv, b_qkv, sin_tab, cos_tab, out_
                 op1=ALU.mult,
             )
 
+        def turned_product_half(block, f, i):
+            w, b = BLOCKS[block]
+            bank = a_psum.tile([P, 2 * P], F32, name="a_bank", tag="a")
+            mx_product(
+                bank[:],
+                lambda g: w_codes[w][0][:, g, f * P:(f + 1) * P],
+                lambda g: w_scales[w][0][:, g, f * P:(f + 1) * P],
+                lambda g: x_codes[:, b, g, 2 * i:2 * i + 2].rearrange("p j r -> p (j r)"),
+                lambda g: x_scales[:, b, g, 2 * i:2 * i + 2].rearrange("p j r -> p (j r)"),
+            )
+            y[(block, f, i)] = y_pool.tile([P, 2, 2 * P], F32, name="y_half", tag="y")
+            nc.vector.scalar_tensor_tensor(
+                out=y[(block, f, i)][:],
+                in0=bank[:].unsqueeze(1).to_broadcast([P, 2, 2 * P]),
+                scalar=turned_bias[:, FT * w + f:FT * w + f + 1],
+                in1=table_T[:, :, 2 * P * i:2 * P * (i + 1)],
+                op0=ALU.add,
+                op1=ALU.mult,
+            )
+
         result = {}
 
         def result_tile(w, b, i):
@@ -224,6 +245,11 @@ def tile_improvedattention_pa_kernel(tc, x, W_qkv, b_qkv, sin_tab, cos_tab, out_
         def heads_of(tile_row, lo, hi):
             return tile_row.rearrange("p (h d) -> p h d", d=D)[:, :, lo:hi]
 
+        def y_columns(block, f, c, j):
+            if (block, f) in y:
+                return y[(block, f)][:, c, j * P:(j + 1) * P]
+            return y[(block, f, j // 2)][:, c, j % 2 * P:(j % 2 + 1) * P]
+
         def turned_back(block, j):
             w, b = BLOCKS[block]
             bank = t_psum.tile([P, FT, P], F32, name="t_bank", tag="t")
@@ -231,7 +257,7 @@ def tile_improvedattention_pa_kernel(tc, x, W_qkv, b_qkv, sin_tab, cos_tab, out_
                 for c, permutation in ((0, ident), (1, swap)):
                     nc.tensor.matmul(
                         out=bank[:, f, :],
-                        lhsT=y[(block, f)][:, c, j * P:(j + 1) * P],
+                        lhsT=y_columns(block, f, c, j),
                         rhs=permutation[:],
                         is_transpose=True,
                         start=(c == 0),
@@ -282,7 +308,6 @@ def tile_improvedattention_pa_kernel(tc, x, W_qkv, b_qkv, sin_tab, cos_tab, out_
             bias = v_bias[:, half * BANK:(half + 1) * BANK]
             add_bias(out, bank[:], bias, direct)
 
-        nc.vector.tensor_copy(out=ident16[:], in_=ident[:])
         for lo, hi in ((0, HALF), (HALF, R)):
             blocks_out = swap[:].rearrange("p (h j) -> p h j", j=R)
             blocks_in = ident[:].rearrange("p (h j) -> p h j", j=R)
@@ -413,6 +438,9 @@ def tile_improvedattention_pa_kernel(tc, x, W_qkv, b_qkv, sin_tab, cos_tab, out_
         v_unit(0, 3, 0, True)
         v_unit(0, 3, 1, False)
         store_row(2, 0, 3)
+        v_unit(1, 0, 0, True)
+        v_unit(1, 0, 1, False)
+        store_row(2, 1, 0)
         passing(2, 0)
         passing(2, 1)
         passing(2, 2)
@@ -423,31 +451,32 @@ def tile_improvedattention_pa_kernel(tc, x, W_qkv, b_qkv, sin_tab, cos_tab, out_
         turned_back(2, 2)
         turned_back(2, 3)
         store(*BLOCKS[2], 1)
-        turned_product(3, 0)
-        turned_product(3, 1)
-        v_unit(1, 0, 0, True)
-        v_unit(1, 0, 1, False)
-        store_row(2, 1, 0)
-        turned_product(3, 2)
-        turned_product(3, 3)
+        turned_product_half(3, 0, 0)
+        turned_product_half(3, 1, 0)
+        turned_product_half(3, 2, 0)
+        turned_product_half(3, 3, 0)
         v_unit(1, 1, 0, True)
         v_unit(1, 1, 1, False)
         store_row(2, 1, 1)
         passing(3, 0)
         passing(3, 1)
-        passing(3, 2)
-        passing(3, 3)
-        v_unit(1, 2, 0, True)
-        v_unit(1, 2, 1, False)
-        store_row(2, 1, 2)
         turned_back(3, 0)
         store_row(*BLOCKS[3], 0)
         turned_back(3, 1)
         store_row(*BLOCKS[3], 1)
-        v_unit(1, 3, 0, True)
-        v_unit(1, 3, 1, True)
-        store_row(2, 1, 3)
+        turned_product_half(3, 0, 1)
+        turned_product_half(3, 1, 1)
+        turned_product_half(3, 2, 1)
+        turned_product_half(3, 3, 1)
+        v_unit(1, 2, 0, True)
+        v_unit(1, 2, 1, False)
+        store_row(2, 1, 2)
+        passing(3, 2)
+        passing(3, 3)
         turned_back(3, 2)
         store_row(*BLOCKS[3], 2)
         turned_back(3, 3)
         store_row(*BLOCKS[3], 3)
+        v_unit(1, 3, 0, True)
+        v_unit(1, 3, 1, True)
+        store_row(2, 1, 3)

@@ -9,7 +9,6 @@ U32 = mybir.dt.uint32
 U8 = mybir.dt.uint8
 FP8X4 = mybir.dt.float8_e4m3fn_x4
 ALU = mybir.AluOpType
-ACT = mybir.ActivationFunctionType
 
 P = 128
 B, S, H, D = 2, 512, 16, 64
@@ -29,16 +28,14 @@ def tile_improvedattention_pa_kernel(tc, x, W_qkv, b_qkv, sin_tab, cos_tab, out_
     nc = tc.nc
     outs = (out_0, out_1, out_2)
     with ExitStack() as ctx:
+        ctx.enter_context(tc.manual_schedule())
         keep = ctx.enter_context(tc.tile_pool(name="keep", bufs=1))
         x_grouped_pool = ctx.enter_context(tc.tile_pool(name="x_grouped", bufs=2))
         w_grouped_pool = ctx.enter_context(tc.tile_pool(name="w_grouped", bufs=3))
         v_grouped_pool = ctx.enter_context(tc.tile_pool(name="v_grouped", bufs=2))
         y_pool = ctx.enter_context(tc.tile_pool(name="y", bufs=10))
-        biased_pool = ctx.enter_context(tc.tile_pool(name="biased", bufs=2))
         result_pool = ctx.enter_context(tc.tile_pool(name="result", bufs=7))
-        a_psum = ctx.enter_context(tc.psum_pool(name="a_psum", bufs=2))
-        t_psum = ctx.enter_context(tc.psum_pool(name="t_psum", bufs=2))
-        p_psum = ctx.enter_context(tc.psum_pool(name="p_psum", bufs=4))
+        psum = ctx.enter_context(tc.psum_pool(name="psum", bufs=8))
 
         x_raw = [[y_pool.tile([P, 2, E], BF16, name="x_raw", tag="y") for i in range(2)] for b in range(B)]
         wq_raw = [[y_pool.tile([P, 4, BANK], BF16, name="wq_raw", tag="y") for g in range(PASSES)] for i in range(2)]
@@ -65,7 +62,9 @@ def tile_improvedattention_pa_kernel(tc, x, W_qkv, b_qkv, sin_tab, cos_tab, out_
         ident = keep.tile([P, P], F32)
         ident16 = keep.tile([P, P], BF16)
         swap = keep.tile([P, P], F32)
+        zeros = keep.tile([P, BANK], BF16)
 
+        nc.vector.memset(zeros[:], 0.0)
         nc.vector.memset(turned_rows[:], 0.0)
         nc.vector.memset(bias_rows[:], 0.0)
         make_identity(nc, ident[:])
@@ -115,7 +114,7 @@ def tile_improvedattention_pa_kernel(tc, x, W_qkv, b_qkv, sin_tab, cos_tab, out_
             grouped = x_grouped_pool.tile([P, PASSES, 2, P, 4], BF16, name="x_grouped", tag="x_grouped", align_bytes=64)
             for jj in range(2):
                 words = x_raw[b][i][:, jj, :].bitcast(F32)
-                bank = p_psum.tile([P, PASSES, 2, P], F32, name="x_bank", tag="p")
+                bank = psum.tile([P, PASSES, 2, P], F32, name="x_bank", tag="bank")
                 for g in range(PASSES):
                     for u in range(2):
                         nc.tensor.transpose(bank[:, g, u, :], words[:, 2 * P * g + u:2 * P * (g + 1):2], ident[:])
@@ -187,9 +186,11 @@ def tile_improvedattention_pa_kernel(tc, x, W_qkv, b_qkv, sin_tab, cos_tab, out_
 
         y = {}
 
-        def turned_product(block, f, direct=True):
+        a_banks = {}
+
+        def turned_product(block, f):
             w, b = BLOCKS[block]
-            bank = a_psum.tile([P, BANK], F32, name="a_bank", tag="a")
+            bank = psum.tile([P, BANK], F32, name="a_bank", tag="bank")
             mx_product(
                 bank[:],
                 lambda g: w_codes[w][0][:, g, f * P:(f + 1) * P],
@@ -197,15 +198,12 @@ def tile_improvedattention_pa_kernel(tc, x, W_qkv, b_qkv, sin_tab, cos_tab, out_
                 lambda g: x_codes[:, b, g].rearrange("p j r -> p (j r)"),
                 lambda g: x_scales[:, b, g].rearrange("p j r -> p (j r)"),
             )
+            a_banks[(block, f)] = bank
+
+        def turned_factors(block, f):
+            w, b = BLOCKS[block]
+            bank = a_banks[(block, f)]
             y[(block, f)] = y_pool.tile([P, 2, BANK], F32, name="y", tag="y")
-            if not direct:
-                biased = biased_pool.tile([P, BANK], F32, name="biased", tag="biased")
-                nc.scalar.activation(
-                    out=biased[:], in_=bank[:], func=ACT.Identity, bias=turned_bias[:, FT * w + f:FT * w + f + 1], scale=1.0
-                )
-                for c in (1, 0):
-                    nc.gpsimd.tensor_tensor(out=y[(block, f)][:, c], in0=biased[:], in1=table_T[:, c], op=ALU.mult)
-                return
             nc.vector.scalar_tensor_tensor(
                 out=y[(block, f)][:],
                 in0=bank[:].unsqueeze(1).to_broadcast([P, 2, BANK]),
@@ -217,7 +215,7 @@ def tile_improvedattention_pa_kernel(tc, x, W_qkv, b_qkv, sin_tab, cos_tab, out_
 
         def turned_product_half(block, f, i):
             w, b = BLOCKS[block]
-            bank = a_psum.tile([P, 2 * P], F32, name="a_bank", tag="a")
+            bank = psum.tile([P, 2 * P], F32, name="a_bank", tag="bank")
             mx_product(
                 bank[:],
                 lambda g: w_codes[w][0][:, g, f * P:(f + 1) * P],
@@ -225,6 +223,11 @@ def tile_improvedattention_pa_kernel(tc, x, W_qkv, b_qkv, sin_tab, cos_tab, out_
                 lambda g: x_codes[:, b, g, 2 * i:2 * i + 2].rearrange("p j r -> p (j r)"),
                 lambda g: x_scales[:, b, g, 2 * i:2 * i + 2].rearrange("p j r -> p (j r)"),
             )
+            a_banks[(block, f, i)] = bank
+
+        def turned_factors_half(block, f, i):
+            w, b = BLOCKS[block]
+            bank = a_banks[(block, f, i)]
             y[(block, f, i)] = y_pool.tile([P, 2, 2 * P], F32, name="y_half", tag="y")
             nc.vector.scalar_tensor_tensor(
                 out=y[(block, f, i)][:],
@@ -245,6 +248,8 @@ def tile_improvedattention_pa_kernel(tc, x, W_qkv, b_qkv, sin_tab, cos_tab, out_
         def heads_of(tile_row, lo, hi):
             return tile_row.rearrange("p (h d) -> p h d", d=D)[:, :, lo:hi]
 
+        t_banks = {}
+
         def y_columns(block, f, c, j):
             if (block, f) in y:
                 return y[(block, f)][:, c, j * P:(j + 1) * P]
@@ -252,7 +257,7 @@ def tile_improvedattention_pa_kernel(tc, x, W_qkv, b_qkv, sin_tab, cos_tab, out_
 
         def turned_back(block, j):
             w, b = BLOCKS[block]
-            bank = t_psum.tile([P, FT, P], F32, name="t_bank", tag="t")
+            bank = psum.tile([P, FT, P], F32, name="t_bank", tag="bank")
             for f in range(FT):
                 for c, permutation in ((0, ident), (1, swap)):
                     nc.tensor.matmul(
@@ -263,9 +268,13 @@ def tile_improvedattention_pa_kernel(tc, x, W_qkv, b_qkv, sin_tab, cos_tab, out_
                         start=(c == 0),
                         stop=(c == 1),
                     )
+            t_banks[(block, j)] = bank
+
+        def turned_out(block, j):
+            w, b = BLOCKS[block]
             nc.scalar.copy(
                 out=heads_of(result_tile(w, b, j // 2)[:, j % 2, :], 0, R),
-                in_=bank[:].rearrange("p f (h j) -> p (f h) j", j=R),
+                in_=t_banks[(block, j)][:].rearrange("p f (h j) -> p (f h) j", j=R),
             )
 
         def store(w, b, i):
@@ -284,7 +293,7 @@ def tile_improvedattention_pa_kernel(tc, x, W_qkv, b_qkv, sin_tab, cos_tab, out_
             nc.sync.dma_start(out=dst[:, j:j + 1, :], in_=result[(w, b, j // 2)][:, j % 2:j % 2 + 1, :])
 
         def row_product(w, part, b, j):
-            bank = p_psum.tile([P, BANK], F32, name="p_bank", tag="p")
+            bank = psum.tile([P, BANK], F32, name="p_bank", tag="bank")
             mx_product(
                 bank[:],
                 lambda g: x_codes[:, b, g, j, :],
@@ -294,16 +303,25 @@ def tile_improvedattention_pa_kernel(tc, x, W_qkv, b_qkv, sin_tab, cos_tab, out_
             )
             return bank
 
-        def passing(block, j, direct=True):
+        row_banks = {}
+
+        def passing_product(block, j):
             w, b = BLOCKS[block]
-            bank = row_product(w, 1, b, j)
+            row_banks[(block, j)] = row_product(w, 1, b, j)
+
+        def passing_out(block, j, direct=True):
+            w, b = BLOCKS[block]
+            bank = row_banks[(block, j)]
             out = heads_of(result_tile(w, b, j // 2)[:, j % 2, :], R, D)
             product = bank[:].rearrange("p (h j) -> p h j", j=R)
             bias = pass_bias[:, w, :].rearrange("p (h j) -> p h j", j=R)
             add_bias(out, product, bias, direct)
 
-        def v_unit(b, j, half, direct):
-            bank = row_product(2, half, b, j)
+        def v_product(b, j, half):
+            row_banks[(b, j, half)] = row_product(2, half, b, j)
+
+        def v_out(b, j, half, direct=True):
+            bank = row_banks[(b, j, half)]
             out = result_tile(2, b, j // 2)[:, j % 2, half * BANK:(half + 1) * BANK]
             bias = v_bias[:, half * BANK:(half + 1) * BANK]
             add_bias(out, bank[:], bias, direct)
@@ -313,7 +331,12 @@ def tile_improvedattention_pa_kernel(tc, x, W_qkv, b_qkv, sin_tab, cos_tab, out_
             blocks_in = ident[:].rearrange("p (h j) -> p h j", j=R)
             nc.vector.tensor_copy(out=blocks_out[:, :, lo:hi], in_=blocks_in[:, :, HALF - lo:HALF - lo + HALF])
 
-        def make_tables():
+        def keep_awake(count):
+            bank = psum.tile([P, BANK], F32, name="awake_bank", tag="bank")
+            for i in range(count):
+                nc.tensor.matmul(out=bank[:], lhsT=zeros[:, 0:P], rhs=zeros[:], start=True, stop=True)
+
+        def make_tables_rows():
             nc.vector.tensor_copy(out=table[:, 0], in_=cos16[:].unsqueeze(2).to_broadcast([P, TILES, 4, R]))
             nc.vector.tensor_copy(
                 out=table[:, 1, :, :, 0:HALF], in_=sin16[:, :, HALF:R].unsqueeze(2).to_broadcast([P, TILES, 4, HALF])
@@ -323,7 +346,9 @@ def tile_improvedattention_pa_kernel(tc, x, W_qkv, b_qkv, sin_tab, cos_tab, out_
                 in0=sin16[:, :, 0:HALF].unsqueeze(2).to_broadcast([P, TILES, 4, HALF]),
                 scalar1=-1.0,
             )
-            table_bank = a_psum.tile([P, 2, TILES, P], BF16, name="table_bank", tag="a")
+
+        def make_tables_columns():
+            table_bank = psum.tile([P, 2, TILES, P], BF16, name="table_bank", tag="bank")
             for c in range(2):
                 for j in range(TILES):
                     nc.tensor.transpose(
@@ -332,12 +357,12 @@ def tile_improvedattention_pa_kernel(tc, x, W_qkv, b_qkv, sin_tab, cos_tab, out_
             nc.scalar.copy(out=table_T[:], in_=table_bank[:].rearrange("p c j r -> p c (j r)"))
 
         def make_turned_bias():
-            rows_bank = a_psum.tile([P, P], BF16, name="rows_bank", tag="a")
+            rows_bank = psum.tile([P, P], BF16, name="rows_bank", tag="bank")
             nc.tensor.transpose(rows_bank[:], turned_rows[:], ident16[:])
             nc.vector.tensor_copy(out=turned_bias[:], in_=rows_bank[:, 0:2 * FT])
 
         def spread_rows(rows, lo, hi, copy_out):
-            bank = p_psum.tile([P, 2 * len(rows), hi - lo], BF16, name="bias_bank", tag="p")
+            bank = psum.tile([P, 2 * len(rows), hi - lo], BF16, name="bias_bank", tag="bank")
             for i, r in enumerate(rows):
                 nc.tensor.matmul(
                     out=bank[:, 2 * i:2 * i + 2, :],
@@ -357,126 +382,198 @@ def tile_improvedattention_pa_kernel(tc, x, W_qkv, b_qkv, sin_tab, cos_tab, out_
 
         v, s = nc.vector.tensor_copy, nc.scalar.copy
         x_grouped = {}
-        make_tables()
+        keep_awake(6)
+        make_tables_rows()
         x_grouped[(0, 0)] = transpose_x(0, 0, (s, v))
+        keep_awake(2)
         regroup_qk(v, 0, 0, 0, wq_raw[0][0][:], 0, HG)
+        make_tables_columns()
         quantise_x(0, 0, x_grouped[(0, 0)])
         x_grouped[(0, 1)] = transpose_x(0, 1, (s, s))
+        keep_awake(2)
         make_turned_bias()
         quantise_half(0, 0, 0, 0)
         regroup_qk(v, 0, 0, 1, wq_raw[0][1][:], 0, HG)
         quantise_x(0, 1, x_grouped[(0, 1)])
         quantise_half(0, 0, 1, 0)
+        regroup_qk(s, 0, 1, 0, wq_raw[0][0][:], 0 * HG, HG)
+        spread_rows(range(0, 16), R, D, pass_bias[:].rearrange("p w c -> p (w c)"))
         turned_product(0, 0)
         turned_product(0, 1)
-        regroup_qk(s, 0, 1, 0, wq_raw[0][0][:], 0 * HG, HG)
-        regroup_qk(s, 0, 1, 1, wq_raw[0][1][:], 0 * HG, HG)
+        turned_factors(0, 0)
+        turned_factors(0, 1)
         regroup_qk(s, 0, 0, 0, wq_raw[1][0][:], HG, HG)
         regroup_qk(v, 0, 0, 1, wq_raw[1][1][:], HG, HG)
         quantise_half(0, 0, 0, 1)
         quantise_half(0, 0, 1, 1)
+        x_grouped[(1, 0)] = transpose_x(1, 0, (s, s))
+        regroup_qk(s, 0, 1, 1, wq_raw[0][1][:], 0 * HG, HG)
+        x_grouped[(1, 1)] = transpose_x(1, 1, (s, s))
         turned_product(0, 2)
         turned_product(0, 3)
-        spread_rows(range(0, 16), R, D, pass_bias[:].rearrange("p w c -> p (w c)"))
-        x_grouped[(1, 0)] = transpose_x(1, 0, (s, s))
-        x_grouped[(1, 1)] = transpose_x(1, 1, (s, s))
-        quantise_x(1, 0, x_grouped[(1, 0)])
-        quantise_x(1, 1, x_grouped[(1, 1)])
+        turned_factors(0, 2)
+        turned_factors(0, 3)
         regroup_qk(s, 0, 1, 0, wq_raw[1][0][:], 1 * HG, HG)
+        quantise_x(1, 0, x_grouped[(1, 0)])
         regroup_qk(v, 0, 1, 1, wq_raw[1][1][:], 1 * HG, HG)
+        quantise_x(1, 1, x_grouped[(1, 1)])
         quantise_w(0, 1)
         turned_back(0, 0)
         turned_back(0, 1)
         turned_product(1, 0)
+        regroup_v(s, 0, 1)
         turned_product(1, 1)
-        passing(0, 0)
-        passing(0, 1)
+        passing_product(0, 0)
+        passing_product(0, 1)
+        turned_factors(1, 0)
+        regroup_v(s, 1, 0)
+        passing_out(0, 0)
+        passing_out(0, 1)
+        turned_out(0, 0)
+        turned_out(0, 1)
         store(*BLOCKS[0], 0)
         turned_back(0, 2)
         turned_back(0, 3)
+        turned_factors(1, 1)
+        passing_product(0, 2)
+        passing_product(0, 3)
         turned_product(1, 2)
-        turned_product(1, 3)
-        passing(0, 2)
-        passing(0, 3)
+        passing_out(0, 2)
+        passing_out(0, 3)
+        turned_out(0, 2)
+        turned_out(0, 3)
         store(*BLOCKS[0], 1)
-        passing(1, 0)
-        passing(1, 1)
-        passing(1, 2)
-        passing(1, 3)
+        turned_product(1, 3)
+        turned_factors(1, 2)
+        passing_product(1, 0)
+        passing_product(1, 1)
+        turned_factors(1, 3)
+        regroup_v(s, 1, 1)
+        passing_product(1, 2)
+        passing_product(1, 3)
+        passing_out(1, 0)
+        passing_out(1, 1)
         turned_back(1, 0)
         turned_back(1, 1)
-        store(*BLOCKS[1], 0)
+        regroup_qk(s, 1, 0, 0, w_raw[1][0][:], 0, H)
+        passing_out(1, 2)
+        passing_out(1, 3)
         turned_back(1, 2)
         turned_back(1, 3)
+        turned_out(1, 0)
+        turned_out(1, 1)
+        store(*BLOCKS[1], 0)
+        turned_out(1, 2)
+        turned_out(1, 3)
         store(*BLOCKS[1], 1)
-        regroup_v(v, 0, 0)
-        regroup_v(s, 0, 1)
-        quantise_w(2, 0)
-        regroup_v(s, 1, 0)
-        regroup_v(s, 1, 1)
-        quantise_w(2, 1)
         spread_rows(range(16, 24), 0, D, v_bias[:])
-        v_unit(0, 0, 0, True)
-        v_unit(0, 0, 1, False)
-        store_row(2, 0, 0)
-        v_unit(0, 1, 0, True)
-        v_unit(0, 1, 1, False)
-        store_row(2, 0, 1)
-        regroup_qk(s, 1, 0, 0, w_raw[1][0][:], 0, H)
         regroup_qk(s, 1, 0, 1, w_raw[1][1][:], 0, H)
+        regroup_v(v, 0, 0)
+        quantise_w(2, 0)
+        quantise_w(2, 1)
+        v_product(0, 0, 0)
+        v_product(0, 1, 0)
+        v_product(0, 2, 0)
+        v_product(0, 0, 1)
+        v_product(0, 1, 1)
+        v_out(0, 0, 0)
+        v_out(0, 1, 0)
+        v_out(0, 2, 0)
+        v_out(0, 0, 1, False)
+        store_row(2, 0, 0)
+        v_out(0, 1, 1, False)
+        store_row(2, 0, 1)
+        v_product(0, 2, 1)
+        v_product(0, 3, 0)
         quantise_w(1, 0)
+        v_out(0, 2, 1, False)
+        store_row(2, 0, 2)
+        v_out(0, 3, 0)
         regroup_qk(s, 1, 1, 0, w_raw[1][0][:], 0, H)
-        regroup_qk(s, 1, 1, 1, w_raw[1][1][:], 0, H)
-        quantise_w(1, 1)
         turned_product(2, 0)
         turned_product(2, 1)
+        v_product(0, 3, 1)
+        turned_factors(2, 0)
         turned_product(2, 2)
+        turned_factors(2, 1)
         turned_product(2, 3)
-        v_unit(0, 2, 0, True)
-        v_unit(0, 2, 1, False)
-        store_row(2, 0, 2)
-        v_unit(0, 3, 0, True)
-        v_unit(0, 3, 1, False)
+        v_out(0, 3, 1, False)
         store_row(2, 0, 3)
-        v_unit(1, 0, 0, True)
-        v_unit(1, 0, 1, False)
+        regroup_qk(s, 1, 1, 1, w_raw[1][1][:], 0, H)
+        v_product(1, 0, 0)
+        v_product(1, 0, 1)
+        v_product(1, 1, 0)
+        turned_factors(2, 2)
+        v_out(1, 0, 0)
+        turned_factors(2, 3)
+        v_out(1, 0, 1, False)
         store_row(2, 1, 0)
-        passing(2, 0)
-        passing(2, 1)
-        passing(2, 2)
-        passing(2, 3)
-        turned_back(2, 0)
-        turned_back(2, 1)
-        store(*BLOCKS[2], 0)
-        turned_back(2, 2)
-        turned_back(2, 3)
-        store(*BLOCKS[2], 1)
+        v_out(1, 1, 0)
         turned_product_half(3, 0, 0)
         turned_product_half(3, 1, 0)
+        turned_back(2, 0)
+        turned_back(2, 1)
+        turned_out(2, 0)
+        turned_out(2, 1)
+        quantise_w(1, 1)
+        turned_back(2, 2)
+        turned_back(2, 3)
+        v_product(1, 1, 1)
+        v_product(1, 2, 0)
+        v_product(1, 2, 1)
+        turned_out(2, 2)
+        turned_out(2, 3)
+        turned_factors_half(3, 0, 0)
+        passing_product(2, 0)
+        passing_product(2, 1)
+        turned_factors_half(3, 1, 0)
+        passing_product(2, 2)
+        passing_product(2, 3)
+        v_out(1, 1, 1, False)
+        store_row(2, 1, 1)
+        v_out(1, 2, 0)
+        v_out(1, 2, 1, False)
+        store_row(2, 1, 2)
+        passing_out(2, 0)
+        passing_out(2, 1)
+        store(*BLOCKS[2], 0)
         turned_product_half(3, 2, 0)
         turned_product_half(3, 3, 0)
-        v_unit(1, 1, 0, True)
-        v_unit(1, 1, 1, False)
-        store_row(2, 1, 1)
-        passing(3, 0)
-        passing(3, 1)
-        turned_back(3, 0)
-        store_row(*BLOCKS[3], 0)
-        turned_back(3, 1)
-        store_row(*BLOCKS[3], 1)
+        passing_out(2, 2)
+        passing_out(2, 3)
+        store(*BLOCKS[2], 1)
+        turned_factors_half(3, 2, 0)
+        turned_factors_half(3, 3, 0)
+        passing_product(3, 0)
+        passing_product(3, 1)
         turned_product_half(3, 0, 1)
         turned_product_half(3, 1, 1)
+        passing_out(3, 0)
+        passing_out(3, 1)
+        turned_back(3, 0)
+        turned_back(3, 1)
+        turned_out(3, 0)
+        store_row(*BLOCKS[3], 0)
+        turned_out(3, 1)
+        store_row(*BLOCKS[3], 1)
+        turned_factors_half(3, 0, 1)
         turned_product_half(3, 2, 1)
         turned_product_half(3, 3, 1)
-        v_unit(1, 2, 0, True)
-        v_unit(1, 2, 1, False)
-        store_row(2, 1, 2)
-        passing(3, 2)
-        passing(3, 3)
+        turned_factors_half(3, 1, 1)
+        passing_product(3, 2)
+        passing_product(3, 3)
+        turned_factors_half(3, 2, 1)
+        turned_factors_half(3, 3, 1)
+        passing_out(3, 2)
         turned_back(3, 2)
-        store_row(*BLOCKS[3], 2)
+        passing_out(3, 3)
         turned_back(3, 3)
+        v_product(1, 3, 0)
+        v_product(1, 3, 1)
+        turned_out(3, 2)
+        store_row(*BLOCKS[3], 2)
+        turned_out(3, 3)
         store_row(*BLOCKS[3], 3)
-        v_unit(1, 3, 0, True)
-        v_unit(1, 3, 1, True)
+        v_out(1, 3, 0)
+        v_out(1, 3, 1, False)
         store_row(2, 1, 3)

from contextlib import ExitStack

import concourse.mybir as mybir
from concourse.masks import make_identity

F32 = mybir.dt.float32
BF16 = mybir.dt.bfloat16
U32 = mybir.dt.uint32
U8 = mybir.dt.uint8
FP8X4 = mybir.dt.float8_e4m3fn_x4
ALU = mybir.AluOpType

P = 128
B, S, H, D = 2, 512, 16, 64
E = H * D
R = D // 2
HALF = R // 2
TILES = S // P
PASSES = E // (4 * P)
BANK = 512
FT = 4
HG = H // 2
FLOPS = 2 * B * S * E * 3 * E
BLOCKS = ((0, 0), (0, 1), (1, 0), (1, 1))


def tile_improvedattention_pa_kernel(tc, x, W_qkv, b_qkv, sin_tab, cos_tab, out_0, out_1, out_2):
    nc = tc.nc
    outs = (out_0, out_1, out_2)
    with ExitStack() as ctx:
        ctx.enter_context(tc.manual_schedule())
        keep = ctx.enter_context(tc.tile_pool(name="keep", bufs=1))
        x_grouped_pool = ctx.enter_context(tc.tile_pool(name="x_grouped", bufs=2))
        w_grouped_pool = ctx.enter_context(tc.tile_pool(name="w_grouped", bufs=3))
        v_grouped_pool = ctx.enter_context(tc.tile_pool(name="v_grouped", bufs=2))
        y_pool = ctx.enter_context(tc.tile_pool(name="y", bufs=10))
        result_pool = ctx.enter_context(tc.tile_pool(name="result", bufs=7))
        psum = ctx.enter_context(tc.psum_pool(name="psum", bufs=8))

        x_raw = [[y_pool.tile([P, 2, E], BF16, name="x_raw", tag="y") for i in range(2)] for b in range(B)]
        wq_raw = [[y_pool.tile([P, 4, BANK], BF16, name="wq_raw", tag="y") for g in range(PASSES)] for i in range(2)]
        w_raw = {w: [keep.tile([P, 4, E], BF16, name="w_raw%d%d" % (w, g)) for g in range(PASSES)] for w in (1, 2)}
        w_codes = [
            [keep.tile([P, PASSES, BANK], U32, name="w_codes%d%d" % (w, i), align_bytes=64) for i in range(2)]
            for w in range(3)
        ]
        w_scales = [
            [keep.tile([P, PASSES, BANK], U8, name="w_scales%d%d" % (w, i), align_bytes=64) for i in range(2)]
            for w in range(3)
        ]
        x_codes = keep.tile([P, B, PASSES, TILES, P], U32, align_bytes=64)
        x_scales = keep.tile([P, B, PASSES, TILES, P], U8, align_bytes=64)
        cos16 = keep.tile([P, TILES, R], BF16)
        sin16 = keep.tile([P, TILES, R], BF16)
        table = keep.tile([P, 2, TILES, 4, R], BF16)
        table_T = keep.tile([P, 2, BANK], BF16)
        bias_rows = keep.tile([P, P], BF16)
        turned_rows = keep.tile([P, P], BF16)
        turned_bias = keep.tile([P, 2 * FT], F32)
        pass_bias = keep.tile([P, 2, BANK], BF16)
        v_bias = keep.tile([P, E], BF16)
        ident = keep.tile([P, P], F32)
        ident16 = keep.tile([P, P], BF16)
        swap = keep.tile([P, P], F32)
        zeros = keep.tile([P, BANK], BF16)

        nc.vector.memset(zeros[:], 0.0)
        nc.vector.memset(turned_rows[:], 0.0)
        nc.vector.memset(bias_rows[:], 0.0)
        make_identity(nc, ident[:])
        make_identity(nc, ident16[:])

        def load_x(b, i):
            src = x[b].rearrange("(p t) k -> p t k", t=TILES)
            nc.sync.dma_start(out=x_raw[b][i][:], in_=src[:, 2 * i:2 * i + 2, :])

        def load_wq(i, g):
            src = W_qkv[4 * P * g:4 * P * (g + 1), i * BANK:(i + 1) * BANK]
            nc.sync.dma_start(out=wq_raw[i][g][:], in_=src.rearrange("(p t) c -> p t c", t=4))

        nc.sync.dma_start(out=cos16[:], in_=cos_tab.rearrange("(p t) j -> p t j", t=TILES))
        nc.sync.dma_start(out=sin16[:], in_=sin_tab.rearrange("(p t) j -> p t j", t=TILES))
        load_x(0, 0)
        load_wq(0, 0)
        load_x(0, 1)
        nc.sync.dma_start(
            out=turned_rows[0:2 * FT, :].rearrange("r (h j) -> r h j", j=R),
            in_=b_qkv[0:2 * E].rearrange("(r h d) -> r h d", h=4, d=D)[:, :, 0:R],
        )
        nc.sync.dma_start(out=bias_rows[0:3 * E // P, :], in_=b_qkv.rearrange("(r c) -> r c", c=P))
        load_wq(0, 1)
        load_wq(1, 0)
        load_wq(1, 1)
        load_x(1, 0)
        load_x(1, 1)
        for w in (2, 1):
            for g in range(PASSES):
                src = W_qkv[4 * P * g:4 * P * (g + 1), w * E:(w + 1) * E]
                nc.sync.dma_start(out=w_raw[w][g][:], in_=src.rearrange("(p t) c -> p t c", t=4))

        def mx_product(out, lhsT, lhsT_scale, rhs, rhs_scale):
            for g in range(PASSES):
                nc.tensor.matmul_mx(
                    out=out,
                    lhsT=lhsT(g).bitcast(FP8X4),
                    lhsT_scale=lhsT_scale(g),
                    rhs=rhs(g).bitcast(FP8X4),
                    rhs_scale=rhs_scale(g),
                    start=(g == 0),
                    stop=(g == PASSES - 1),
                )

        def transpose_x(b, i, copies):
            grouped = x_grouped_pool.tile([P, PASSES, 2, P, 4], BF16, name="x_grouped", tag="x_grouped", align_bytes=64)
            for jj in range(2):
                words = x_raw[b][i][:, jj, :].bitcast(F32)
                bank = psum.tile([P, PASSES, 2, P], F32, name="x_bank", tag="bank")
                for g in range(PASSES):
                    for u in range(2):
                        nc.tensor.transpose(bank[:, g, u, :], words[:, 2 * P * g + u:2 * P * (g + 1):2], ident[:])
                copies[jj](
                    out=grouped[:, :, jj].rearrange("p g r t -> p g (r t)").bitcast(F32).rearrange("p g (r u) -> p g r u", u=2),
                    in_=bank[:].rearrange("p g u r -> p g r u"),
                )
            return grouped

        def quantise_x(b, i, grouped):
            for g in range(PASSES):
                nc.vector.quantize_mx(
                    out=x_codes[:, b, g, 2 * i:2 * i + 2, :].rearrange("p j r -> p (j r)").bitcast(FP8X4),
                    scales=x_scales[:, b, g, 2 * i:2 * i + 2, :].rearrange("p j r -> p (j r)"),
                    in_=grouped[:, g].rearrange("p j r t -> p (j r t)"),
                )

        w_grouped = {}

        def grouped_tile(w, part, g):
            if (w, part) not in w_grouped:
                pool = v_grouped_pool if w == 2 else w_grouped_pool
                w_grouped[(w, part)] = pool.tile(
                    [P, PASSES, BANK, 4], BF16, name="w_grouped", tag="w_grouped", align_bytes=64
                )
            return w_grouped[(w, part)][:, g]

        def regroup_qk(copy, w, part, g, source, first_head, heads):
            dst = grouped_tile(w, part, g)[:, first_head * R:(first_head + heads) * R, :]
            src = source.rearrange("p t (h e c i) -> p h e c t i", e=2, c=R // 4, i=4)
            copy(out=dst.rearrange("p (h c i) t -> p h c t i", c=R // 4, i=4), in_=src[:, :, part])

        def regroup_v(copy, part, g):
            src = w_raw[2][g][:, :, part * BANK:(part + 1) * BANK]
            copy(
                out=grouped_tile(2, part, g).rearrange("p (c i) t -> p c t i", i=4),
                in_=src.rearrange("p t (c i) -> p c t i", i=4),
            )

        def regroup_on_gpsimd(w, part, g, source, first, count, pieces):
            width = count // pieces
            for c0 in range(first, first + count, width):
                dst = grouped_tile(w, part, g)[:, c0:c0 + width, :]
                if w == 2:
                    src = source[:, :, c0 - first:c0 - first + width].rearrange("p t c -> p c t")
                else:
                    src = heads_of_rows(source, (c0 - first) // R, width // R, part)
                    dst = dst.rearrange("p (h j) t -> p h j t", j=R)
                nc.gpsimd.tensor_scalar(out=dst, in0=src, scalar1=1.0, scalar2=0.0, op0=ALU.mult, op1=ALU.add)

        def heads_of_rows(source, first_head, heads, part):
            rows = source.rearrange("p t (h e j) -> p h e j t", e=2, j=R)
            return rows[:, first_head:first_head + heads, part]

        def quantise_w(w, part):
            nc.vector.quantize_mx(
                out=w_codes[w][part][:].rearrange("p g c -> p (g c)").bitcast(FP8X4),
                scales=w_scales[w][part][:].rearrange("p g c -> p (g c)"),
                in_=w_grouped[(w, part)][:].rearrange("p g c t -> p (g c t)"),
            )

        def quantise_half(w, part, g, half):
            c0 = half * HG * R
            nc.vector.quantize_mx(
                out=w_codes[w][part][:, g, c0:c0 + HG * R].bitcast(FP8X4),
                scales=w_scales[w][part][:, g, c0:c0 + HG * R],
                in_=w_grouped[(w, part)][:, g, c0:c0 + HG * R, :].rearrange("p c t -> p (c t)"),
            )

        y = {}

        a_banks = {}

        def turned_product(block, f):
            w, b = BLOCKS[block]
            bank = psum.tile([P, BANK], F32, name="a_bank", tag="bank")
            mx_product(
                bank[:],
                lambda g: w_codes[w][0][:, g, f * P:(f + 1) * P],
                lambda g: w_scales[w][0][:, g, f * P:(f + 1) * P],
                lambda g: x_codes[:, b, g].rearrange("p j r -> p (j r)"),
                lambda g: x_scales[:, b, g].rearrange("p j r -> p (j r)"),
            )
            a_banks[(block, f)] = bank

        def turned_factors(block, f):
            w, b = BLOCKS[block]
            bank = a_banks[(block, f)]
            y[(block, f)] = y_pool.tile([P, 2, BANK], F32, name="y", tag="y")
            nc.vector.scalar_tensor_tensor(
                out=y[(block, f)][:],
                in0=bank[:].unsqueeze(1).to_broadcast([P, 2, BANK]),
                scalar=turned_bias[:, FT * w + f:FT * w + f + 1],
                in1=table_T[:],
                op0=ALU.add,
                op1=ALU.mult,
            )

        def turned_product_half(block, f, i):
            w, b = BLOCKS[block]
            bank = psum.tile([P, 2 * P], F32, name="a_bank", tag="bank")
            mx_product(
                bank[:],
                lambda g: w_codes[w][0][:, g, f * P:(f + 1) * P],
                lambda g: w_scales[w][0][:, g, f * P:(f + 1) * P],
                lambda g: x_codes[:, b, g, 2 * i:2 * i + 2].rearrange("p j r -> p (j r)"),
                lambda g: x_scales[:, b, g, 2 * i:2 * i + 2].rearrange("p j r -> p (j r)"),
            )
            a_banks[(block, f, i)] = bank

        def turned_factors_half(block, f, i):
            w, b = BLOCKS[block]
            bank = a_banks[(block, f, i)]
            y[(block, f, i)] = y_pool.tile([P, 2, 2 * P], F32, name="y_half", tag="y")
            nc.vector.scalar_tensor_tensor(
                out=y[(block, f, i)][:],
                in0=bank[:].unsqueeze(1).to_broadcast([P, 2, 2 * P]),
                scalar=turned_bias[:, FT * w + f:FT * w + f + 1],
                in1=table_T[:, :, 2 * P * i:2 * P * (i + 1)],
                op0=ALU.add,
                op1=ALU.mult,
            )

        result = {}

        def result_tile(w, b, i):
            if (w, b, i) not in result:
                result[(w, b, i)] = result_pool.tile([P, 2, E], F32, name="result", tag="result")
            return result[(w, b, i)]

        def heads_of(tile_row, lo, hi):
            return tile_row.rearrange("p (h d) -> p h d", d=D)[:, :, lo:hi]

        t_banks = {}

        def y_columns(block, f, c, j):
            if (block, f) in y:
                return y[(block, f)][:, c, j * P:(j + 1) * P]
            return y[(block, f, j // 2)][:, c, j % 2 * P:(j % 2 + 1) * P]

        def turned_back(block, j):
            w, b = BLOCKS[block]
            bank = psum.tile([P, FT, P], F32, name="t_bank", tag="bank")
            for f in range(FT):
                for c, permutation in ((0, ident), (1, swap)):
                    nc.tensor.matmul(
                        out=bank[:, f, :],
                        lhsT=y_columns(block, f, c, j),
                        rhs=permutation[:],
                        is_transpose=True,
                        start=(c == 0),
                        stop=(c == 1),
                    )
            t_banks[(block, j)] = bank

        def turned_out(block, j):
            w, b = BLOCKS[block]
            nc.scalar.copy(
                out=heads_of(result_tile(w, b, j // 2)[:, j % 2, :], 0, R),
                in_=t_banks[(block, j)][:].rearrange("p f (h j) -> p (f h) j", j=R),
            )

        def store(w, b, i):
            dst = outs[w][b].rearrange("(p t) h d -> p t (h d)", t=TILES)
            nc.sync.dma_start(out=dst[:, 2 * i:2 * i + 2, :], in_=result[(w, b, i)][:])

        def add_bias(out, product, bias, direct):
            if direct:
                nc.vector.tensor_tensor(out=out, in0=product, in1=bias, op=ALU.add)
            else:
                nc.scalar.copy(out=out, in_=product)
                nc.gpsimd.tensor_tensor(out=out, in0=out, in1=bias, op=ALU.add)

        def store_row(w, b, j):
            dst = outs[w][b].rearrange("(p t) h d -> p t (h d)", t=TILES)
            nc.sync.dma_start(out=dst[:, j:j + 1, :], in_=result[(w, b, j // 2)][:, j % 2:j % 2 + 1, :])

        def row_product(w, part, b, j):
            bank = psum.tile([P, BANK], F32, name="p_bank", tag="bank")
            mx_product(
                bank[:],
                lambda g: x_codes[:, b, g, j, :],
                lambda g: x_scales[:, b, g, j, :],
                lambda g: w_codes[w][part][:, g, :],
                lambda g: w_scales[w][part][:, g, :],
            )
            return bank

        row_banks = {}

        def passing_product(block, j):
            w, b = BLOCKS[block]
            row_banks[(block, j)] = row_product(w, 1, b, j)

        def passing_out(block, j, direct=True):
            w, b = BLOCKS[block]
            bank = row_banks[(block, j)]
            out = heads_of(result_tile(w, b, j // 2)[:, j % 2, :], R, D)
            product = bank[:].rearrange("p (h j) -> p h j", j=R)
            bias = pass_bias[:, w, :].rearrange("p (h j) -> p h j", j=R)
            add_bias(out, product, bias, direct)

        def v_product(b, j, half):
            row_banks[(b, j, half)] = row_product(2, half, b, j)

        def v_out(b, j, half, direct=True):
            bank = row_banks[(b, j, half)]
            out = result_tile(2, b, j // 2)[:, j % 2, half * BANK:(half + 1) * BANK]
            bias = v_bias[:, half * BANK:(half + 1) * BANK]
            add_bias(out, bank[:], bias, direct)

        for lo, hi in ((0, HALF), (HALF, R)):
            blocks_out = swap[:].rearrange("p (h j) -> p h j", j=R)
            blocks_in = ident[:].rearrange("p (h j) -> p h j", j=R)
            nc.vector.tensor_copy(out=blocks_out[:, :, lo:hi], in_=blocks_in[:, :, HALF - lo:HALF - lo + HALF])

        def keep_awake(count):
            bank = psum.tile([P, BANK], F32, name="awake_bank", tag="bank")
            for i in range(count):
                nc.tensor.matmul(out=bank[:], lhsT=zeros[:, 0:P], rhs=zeros[:], start=True, stop=True)

        def make_tables_rows():
            nc.vector.tensor_copy(out=table[:, 0], in_=cos16[:].unsqueeze(2).to_broadcast([P, TILES, 4, R]))
            nc.vector.tensor_copy(
                out=table[:, 1, :, :, 0:HALF], in_=sin16[:, :, HALF:R].unsqueeze(2).to_broadcast([P, TILES, 4, HALF])
            )
            nc.vector.tensor_scalar_mul(
                out=table[:, 1, :, :, HALF:R],
                in0=sin16[:, :, 0:HALF].unsqueeze(2).to_broadcast([P, TILES, 4, HALF]),
                scalar1=-1.0,
            )

        def make_tables_columns():
            table_bank = psum.tile([P, 2, TILES, P], BF16, name="table_bank", tag="bank")
            for c in range(2):
                for j in range(TILES):
                    nc.tensor.transpose(
                        table_bank[:, c, j, :], table[:, c, j].rearrange("p h j -> p (h j)"), ident16[:]
                    )
            nc.scalar.copy(out=table_T[:], in_=table_bank[:].rearrange("p c j r -> p c (j r)"))

        def make_turned_bias():
            rows_bank = psum.tile([P, P], BF16, name="rows_bank", tag="bank")
            nc.tensor.transpose(rows_bank[:], turned_rows[:], ident16[:])
            nc.vector.tensor_copy(out=turned_bias[:], in_=rows_bank[:, 0:2 * FT])

        def spread_rows(rows, lo, hi, copy_out):
            bank = psum.tile([P, 2 * len(rows), hi - lo], BF16, name="bias_bank", tag="bank")
            for i, r in enumerate(rows):
                nc.tensor.matmul(
                    out=bank[:, 2 * i:2 * i + 2, :],
                    lhsT=ident16[:, r:r + 1].to_broadcast([P, P]),
                    rhs=heads_of(bias_rows[:], lo, hi),
                    start=True,
                    stop=True,
                )
            nc.scalar.copy(out=copy_out, in_=bank[:].rearrange("p h j -> p (h j)"))

        def finish(block, i, complete=True):
            w, b = BLOCKS[block]
            for j in (2 * i, 2 * i + 1):
                turned_back(block, j)
            if complete:
                store(w, b, i)

        v, s = nc.vector.tensor_copy, nc.scalar.copy
        x_grouped = {}
        keep_awake(6)
        make_tables_rows()
        x_grouped[(0, 0)] = transpose_x(0, 0, (s, v))
        keep_awake(2)
        regroup_qk(v, 0, 0, 0, wq_raw[0][0][:], 0, HG)
        make_tables_columns()
        quantise_x(0, 0, x_grouped[(0, 0)])
        x_grouped[(0, 1)] = transpose_x(0, 1, (s, s))
        keep_awake(2)
        make_turned_bias()
        quantise_half(0, 0, 0, 0)
        regroup_qk(v, 0, 0, 1, wq_raw[0][1][:], 0, HG)
        quantise_x(0, 1, x_grouped[(0, 1)])
        quantise_half(0, 0, 1, 0)
        regroup_qk(s, 0, 1, 0, wq_raw[0][0][:], 0 * HG, HG)
        spread_rows(range(0, 16), R, D, pass_bias[:].rearrange("p w c -> p (w c)"))
        turned_product(0, 0)
        turned_product(0, 1)
        turned_factors(0, 0)
        turned_factors(0, 1)
        regroup_qk(s, 0, 0, 0, wq_raw[1][0][:], HG, HG)
        regroup_qk(v, 0, 0, 1, wq_raw[1][1][:], HG, HG)
        quantise_half(0, 0, 0, 1)
        quantise_half(0, 0, 1, 1)
        x_grouped[(1, 0)] = transpose_x(1, 0, (s, s))
        regroup_qk(s, 0, 1, 1, wq_raw[0][1][:], 0 * HG, HG)
        x_grouped[(1, 1)] = transpose_x(1, 1, (s, s))
        turned_product(0, 2)
        turned_product(0, 3)
        turned_factors(0, 2)
        turned_factors(0, 3)
        regroup_qk(s, 0, 1, 0, wq_raw[1][0][:], 1 * HG, HG)
        quantise_x(1, 0, x_grouped[(1, 0)])
        regroup_qk(v, 0, 1, 1, wq_raw[1][1][:], 1 * HG, HG)
        quantise_x(1, 1, x_grouped[(1, 1)])
        quantise_w(0, 1)
        turned_back(0, 0)
        turned_back(0, 1)
        turned_product(1, 0)
        regroup_v(s, 0, 1)
        turned_product(1, 1)
        passing_product(0, 0)
        passing_product(0, 1)
        turned_factors(1, 0)
        regroup_v(s, 1, 0)
        passing_out(0, 0)
        passing_out(0, 1)
        turned_out(0, 0)
        turned_out(0, 1)
        store(*BLOCKS[0], 0)
        turned_back(0, 2)
        turned_back(0, 3)
        turned_factors(1, 1)
        passing_product(0, 2)
        passing_product(0, 3)
        turned_product(1, 2)
        passing_out(0, 2)
        passing_out(0, 3)
        turned_out(0, 2)
        turned_out(0, 3)
        store(*BLOCKS[0], 1)
        turned_product(1, 3)
        turned_factors(1, 2)
        passing_product(1, 0)
        passing_product(1, 1)
        turned_factors(1, 3)
        regroup_v(s, 1, 1)
        passing_product(1, 2)
        passing_product(1, 3)
        passing_out(1, 0)
        passing_out(1, 1)
        turned_back(1, 0)
        turned_back(1, 1)
        regroup_qk(s, 1, 0, 0, w_raw[1][0][:], 0, H)
        passing_out(1, 2)
        passing_out(1, 3)
        turned_back(1, 2)
        turned_back(1, 3)
        turned_out(1, 0)
        turned_out(1, 1)
        store(*BLOCKS[1], 0)
        turned_out(1, 2)
        turned_out(1, 3)
        store(*BLOCKS[1], 1)
        spread_rows(range(16, 24), 0, D, v_bias[:])
        regroup_qk(s, 1, 0, 1, w_raw[1][1][:], 0, H)
        regroup_v(v, 0, 0)
        quantise_w(2, 0)
        quantise_w(2, 1)
        v_product(0, 0, 0)
        v_product(0, 1, 0)
        v_product(0, 2, 0)
        v_product(0, 0, 1)
        v_product(0, 1, 1)
        v_out(0, 0, 0)
        v_out(0, 1, 0)
        v_out(0, 2, 0)
        v_out(0, 0, 1, False)
        store_row(2, 0, 0)
        v_out(0, 1, 1, False)
        store_row(2, 0, 1)
        v_product(0, 2, 1)
        v_product(0, 3, 0)
        quantise_w(1, 0)
        v_out(0, 2, 1, False)
        store_row(2, 0, 2)
        v_out(0, 3, 0)
        regroup_qk(s, 1, 1, 0, w_raw[1][0][:], 0, H)
        turned_product(2, 0)
        turned_product(2, 1)
        v_product(0, 3, 1)
        turned_factors(2, 0)
        turned_product(2, 2)
        turned_factors(2, 1)
        turned_product(2, 3)
        v_out(0, 3, 1, False)
        store_row(2, 0, 3)
        regroup_qk(s, 1, 1, 1, w_raw[1][1][:], 0, H)
        v_product(1, 0, 0)
        v_product(1, 0, 1)
        v_product(1, 1, 0)
        turned_factors(2, 2)
        v_out(1, 0, 0)
        turned_factors(2, 3)
        v_out(1, 0, 1, False)
        store_row(2, 1, 0)
        v_out(1, 1, 0)
        turned_product_half(3, 0, 0)
        turned_product_half(3, 1, 0)
        turned_back(2, 0)
        turned_back(2, 1)
        turned_out(2, 0)
        turned_out(2, 1)
        quantise_w(1, 1)
        turned_back(2, 2)
        turned_back(2, 3)
        v_product(1, 1, 1)
        v_product(1, 2, 0)
        v_product(1, 2, 1)
        turned_out(2, 2)
        turned_out(2, 3)
        turned_factors_half(3, 0, 0)
        passing_product(2, 0)
        passing_product(2, 1)
        turned_factors_half(3, 1, 0)
        passing_product(2, 2)
        passing_product(2, 3)
        v_out(1, 1, 1, False)
        store_row(2, 1, 1)
        v_out(1, 2, 0)
        v_out(1, 2, 1, False)
        store_row(2, 1, 2)
        passing_out(2, 0)
        passing_out(2, 1)
        store(*BLOCKS[2], 0)
        turned_product_half(3, 2, 0)
        turned_product_half(3, 3, 0)
        passing_out(2, 2)
        passing_out(2, 3)
        store(*BLOCKS[2], 1)
        turned_factors_half(3, 2, 0)
        turned_factors_half(3, 3, 0)
        passing_product(3, 0)
        passing_product(3, 1)
        turned_product_half(3, 0, 1)
        turned_product_half(3, 1, 1)
        passing_out(3, 0)
        passing_out(3, 1)
        turned_back(3, 0)
        turned_back(3, 1)
        turned_out(3, 0)
        store_row(*BLOCKS[3], 0)
        turned_out(3, 1)
        store_row(*BLOCKS[3], 1)
        turned_factors_half(3, 0, 1)
        turned_product_half(3, 2, 1)
        turned_product_half(3, 3, 1)
        turned_factors_half(3, 1, 1)
        passing_product(3, 2)
        passing_product(3, 3)
        turned_factors_half(3, 2, 1)
        turned_factors_half(3, 3, 1)
        passing_out(3, 2)
        turned_back(3, 2)
        passing_out(3, 3)
        turned_back(3, 3)
        v_product(1, 3, 0)
        v_product(1, 3, 1)
        turned_out(3, 2)
        store_row(*BLOCKS[3], 2)
        turned_out(3, 3)
        store_row(*BLOCKS[3], 3)
        v_out(1, 3, 0)
        v_out(1, 3, 1, False)
        store_row(2, 1, 3)
